import numpy as np
import ml_dtypes

BF16 = ml_dtypes.bfloat16


def bf(x):
    return np.asarray(x, np.float32).astype(BF16)


def f32(x):
    return np.asarray(x, np.float32)


def f64(x):
    return np.asarray(x).astype(np.float64)


def striped(idx):
    return np.tile(idx.reshape(-1, 16).T, (8, 1))


D, C, S, B, L, N, M = 128, 384, 4096, 128, 32, 4096, 128
LN_EPS = 1e-5


def setup_inputs():
    sc = np.repeat([1.0, 0.4, 0.4], D)[:, None]
    return {"tab": f32(sc * np.random.standard_normal((C, S))), "mask": f32(np.random.uniform(0.5, 1.5, (1, N))), "wdec": bf(np.random.standard_normal((D, M)) / np.sqrt(D)), "offs": striped(np.random.permutation(np.tile(np.arange(S), 2))[:N])}


def reference(tab, mask, wdec, offs):
    idx = offs[:16].T.reshape(-1)
    m = f64(mask)
    e = f64(tab)[:, idx] * m
    v, k, q = e.reshape(C // D, D, B, L)
    mb = m.reshape(B, L)
    ksum = k.sum(axis=2)
    s = (q * ksum[:, :, None]).sum(axis=0) / np.sqrt(D)
    y = np.exp(s) * mb
    a = y / y.sum(axis=1, keepdims=True)
    h = (v * a[None]).sum(axis=2) + v.sum(axis=2) / mb.sum(axis=1)[None, :]
    mu = h.mean(axis=0, keepdims=True)
    var = ((h - mu) ** 2).mean(axis=0, keepdims=True)
    z = (h - mu) / np.sqrt(var + LN_EPS)
    return f64(wdec).T @ z

@@ -1,0 +1,194 @@
+import math
+
+import concourse.mybir as mybir
+from concourse.masks import make_identity
+
+F32, BF16, U16 = mybir.dt.float32, mybir.dt.bfloat16, mybir.dt.uint16
+ALU = mybir.AluOpType
+ACT = mybir.ActivationFunctionType
+AX = mybir.AxisListType
+
+P = 128
+S = 4096
+N = 4096
+L = 32
+B = N // L
+PIECE = 512
+N_PIECES = N // PIECE
+BLOCK = P
+SEQ_PER_BLOCK = BLOCK // L
+N_BLOCKS = N // BLOCK
+BLOCKS_PER_PIECE = PIECE // BLOCK
+LN_EPS = 1e-5
+
+FLOPS = 2 * P * P * B + 2 * P * N + 2 * P * N
+
+
+def tile_scaleddpattention_kernel(tc, tab, mask, wdec, offs, out):
+    nc = tc.nc
+    with (
+        tc.tile_pool(name="held", bufs=1) as held,
+        tc.tile_pool(name="ring", bufs=3) as ring,
+        tc.psum_pool(name="psum_held", bufs=1) as psum_held,
+        tc.psum_pool(name="psum_ring", bufs=2) as psum_ring,
+    ):
+        offsets = held.tile([P, N // 16], U16, name="offsets")
+        nc.sync.dma_start(offsets[:], offs)
+
+        mask_row = mask.rearrange("o n -> (o n)")
+        mask_bc = [held.tile([P, PIECE], F32, name=f"mask_bc{i}") for i in range(N_PIECES)]
+        table = {}
+        for name in ("v", "k", "q"):
+            table[name] = held.tile([P, S], F32, name=f"table_{name}")
+
+        def load_mask_piece(i):
+            queue = nc.sync if i % 2 == 0 else nc.scalar
+            queue.dma_start(mask_bc[i][:], mask_row[i * PIECE : (i + 1) * PIECE].partition_broadcast(P))
+
+        def load_table(name, first_row):
+            half = S // 2
+            nc.sync.dma_start(table[name][:, :half], tab[first_row : first_row + P, :half])
+            nc.scalar.dma_start(table[name][:, half:], tab[first_row : first_row + P, half:])
+
+        load_mask_piece(0)
+        load_table("k", P)
+        for i in range(1, N_PIECES):
+            load_mask_piece(i)
+        mask_seq = held.tile([B, L], F32, name="mask_seq")
+        nc.scalar.dma_start(mask_seq[:], mask.rearrange("o (b t) -> (o b) t", t=L))
+        load_table("q", 2 * P)
+        load_table("v", 0)
+        wdec_sb = held.tile([P, P], BF16, name="wdec_sb")
+        nc.scalar.dma_start(wdec_sb[:], wdec)
+
+        ident = held.tile([P, P], F32, name="ident")
+        make_identity(nc, ident[:])
+        ident_bf = held.tile([P, P], BF16, name="ident_bf")
+        nc.vector.tensor_copy(ident_bf[:], ident[:])
+        quarter = held.tile([P, SEQ_PER_BLOCK], F32, name="quarter")
+        nc.vector.reduce_sum(out=quarter[:], in_=ident[:].rearrange("p (c t) -> p c t", t=L), axis=AX.X)
+        nc.vector.tensor_scalar_mul(quarter[:], quarter[:], 1.0 / math.sqrt(P))
+        place = held.tile([P, L], F32, name="place")
+        nc.vector.reduce_sum(out=place[:], in_=ident[:].rearrange("p (c t) -> p t c", t=L), axis=AX.X)
+        slot = held.tile([B, SEQ_PER_BLOCK], F32, name="slot")
+        nc.vector.reduce_sum(
+            out=slot[:], in_=ident[:].rearrange("p (k c) -> p c k", c=SEQ_PER_BLOCK), axis=AX.X
+        )
+        slot_wide = slot[:].unsqueeze(2).to_broadcast([B, SEQ_PER_BLOCK, L])
+        minus_half = held.tile([B, 1], F32, name="minus_half")
+        nc.vector.memset(minus_half[:], -0.5)
+        DIAG = P + SEQ_PER_BLOCK
+        weights = held.tile([P, N_BLOCKS * DIAG], F32, name="weights")
+        nc.gpsimd.memset(weights[:], 0.0)
+
+        mask_sum = held.tile([B, 1], F32, name="mask_sum")
+        nc.vector.reduce_sum(out=mask_sum[:], in_=mask_seq[:], axis=AX.X)
+        mean_weight = held.tile([B, 1], F32, name="mean_weight")
+        nc.vector.reciprocal(mean_weight[:], mask_sum[:])
+        mask_wide = held.tile([B, SEQ_PER_BLOCK, L], F32, name="mask_wide")
+        nc.vector.tensor_tensor(
+            mask_wide[:], mask_seq[:].unsqueeze(1).to_broadcast([B, SEQ_PER_BLOCK, L]), slot_wide, ALU.mult
+        )
+        mean_wide = held.tile([B, SEQ_PER_BLOCK, L], F32, name="mean_wide")
+        nc.vector.tensor_scalar_mul(mean_wide[:], slot_wide, mean_weight[:])
+
+        def look_up(name, i):
+            e = ring.tile([P, PIECE], F32, name=f"e_{name}")
+            picked = table[name][:].indirect(offsets[:, i * PIECE // 16 : (i + 1) * PIECE // 16])
+            nc.vector.tensor_tensor(e[:], picked, mask_bc[i][:], ALU.mult)
+            return e
+
+        ksum = held.tile([P, B], F32, name="ksum")
+        seq_per_piece = PIECE // L
+        for i in range(N_PIECES):
+            k = look_up("k", i)
+            nc.vector.reduce_sum(
+                out=ksum[:, i * seq_per_piece : (i + 1) * seq_per_piece],
+                in_=k[:].rearrange("d (b t) -> d b t", t=L),
+                axis=AX.X,
+            )
+
+        cross_ps = psum_held.tile([P, B], F32, name="cross_ps")
+        for i in range(N_PIECES):
+            q = look_up("q", i)
+            for j in range(BLOCKS_PER_PIECE):
+                block = i * BLOCKS_PER_PIECE + j
+                own = slice(block * SEQ_PER_BLOCK, (block + 1) * SEQ_PER_BLOCK)
+                nc.tensor.matmul(
+                    cross_ps[:, own], lhsT=q[:, j * BLOCK : (j + 1) * BLOCK], rhs=ksum[:, own], start=True, stop=True
+                )
+
+        own_score = held.tile([P, B], F32, name="own_score")
+        nc.vector.tensor_tensor(
+            own_score[:].rearrange("p (k c) -> p k c", c=SEQ_PER_BLOCK),
+            cross_ps[:].rearrange("p (k c) -> p k c", c=SEQ_PER_BLOCK),
+            quarter[:].unsqueeze(1).to_broadcast([P, N_BLOCKS, SEQ_PER_BLOCK]),
+            ALU.mult,
+        )
+        s_ps = psum_held.tile([B, L], F32, name="s_ps")
+        nc.tensor.matmul(s_ps[:], lhsT=own_score[:], rhs=place[:], start=True, stop=True)
+        neg_max = held.tile([B, 1], F32, name="neg_max")
+        nc.vector.reduce_max(out=neg_max[:], in_=s_ps[:], axis=AX.X, negate=True)
+        expd = held.tile([B, L], F32, name="expd")
+        nc.scalar.activation(out=expd[:], in_=s_ps[:], func=ACT.Exp, bias=neg_max[:], scale=1.0)
+        y_wide = held.tile([B, SEQ_PER_BLOCK, L], F32, name="y_wide")
+        nc.vector.tensor_tensor(
+            y_wide[:], expd[:].unsqueeze(1).to_broadcast([B, SEQ_PER_BLOCK, L]), mask_wide[:], ALU.mult
+        )
+        y_sum = held.tile([B, 1], F32, name="y_sum")
+        nc.vector.reduce_sum(out=y_sum[:], in_=y_wide[:].rearrange("b c t -> b (c t)"), axis=AX.X)
+        y_scale = held.tile([B, 1], F32, name="y_scale")
+        nc.vector.reciprocal(y_scale[:], y_sum[:])
+        pool_wide = held.tile([B, P], F32, name="pool_wide")
+        nc.vector.scalar_tensor_tensor(
+            out=pool_wide[:],
+            in0=y_wide[:].rearrange("b c t -> b (c t)"),
+            scalar=y_scale[:],
+            in1=mean_wide[:].rearrange("b c t -> b (c t)"),
+            op0=ALU.mult,
+            op1=ALU.add,
+        )
+        pool_ps = psum_held.tile([P, B], F32, name="pool_ps")
+        nc.tensor.transpose(pool_ps[:], pool_wide[:], ident[:])
+        nc.scalar.copy(
+            weights[:].rearrange("p (k s) -> p k s", s=DIAG)[:, :, :SEQ_PER_BLOCK],
+            pool_ps[:].rearrange("p (k c) -> p k c", c=SEQ_PER_BLOCK),
+        )
+
+        h_ps = psum_held.tile([B, P], F32, name="h_ps")
+        for i in range(N_PIECES):
+            v = look_up("v", i)
+            vT_ps = psum_ring.tile([P, PIECE], F32, name="vT_ps")
+            for j in range(BLOCKS_PER_PIECE):
+                nc.tensor.transpose(vT_ps[:, j * P : (j + 1) * P], v[:, j * BLOCK : (j + 1) * BLOCK], ident[:])
+            vT = ring.tile([P, PIECE], F32, name="vT")
+            nc.scalar.copy(vT[:], vT_ps[:])
+            for j in range(BLOCKS_PER_PIECE):
+                block = i * BLOCKS_PER_PIECE + j
+                nc.tensor.matmul(
+                    h_ps[:],
+                    lhsT=weights[:, block * P : (block + 1) * P],
+                    rhs=vT[:, j * P : (j + 1) * P],
+                    start=(block == 0),
+                    stop=(block == N_BLOCKS - 1),
+                )
+
+        stats = held.tile([B, 6], F32, name="stats")
+        nc.vector.bn_stats(stats[:], h_ps[:])
+        mean_var = held.tile([B, 2], F32, name="mean_var")
+        nc.vector.bn_aggr(mean_var[:], stats[:])
+        var_eps = held.tile([B, 1], F32, name="var_eps")
+        nc.vector.tensor_scalar_add(var_eps[:], mean_var[:, 1:2], LN_EPS)
+        rstd = held.tile([B, 1], F32, name="rstd")
+        nc.gpsimd.tensor_tensor(rstd[:], var_eps[:], minus_half[:], ALU.pow)
+        zT = held.tile([B, P], BF16, name="zT")
+        nc.vector.tensor_scalar(zT[:], h_ps[:], mean_var[:, 0:1], rstd[:], op0=ALU.subtract, op1=ALU.mult)
+        z_ps = psum_held.tile([P, B], BF16, name="z_ps")
+        nc.tensor.transpose(z_ps[:], zT[:], ident_bf[:])
+        z = held.tile([P, B], BF16, name="z")
+        nc.vector.tensor_copy(z[:], z_ps[:])
+        out_ps = psum_held.tile([P, B], F32, name="out_ps")
+        nc.tensor.matmul(out_ps[:], lhsT=wdec_sb[:], rhs=z[:], start=True, stop=True)
+        out_sb = held.tile([P, B], F32, name="out_sb")
+        nc.vector.tensor_copy(out_sb[:], out_ps[:])
+        nc.sync.dma_start(out, out_sb[:])

@@ -14,14 +14,20 @@ N = 4096
 L = 32
 B = N // L
 PIECE = 512
-N_PIECES = N // PIECE
+NI = N // PIECE
 BLOCK = P
-SEQ_PER_BLOCK = BLOCK // L
-N_BLOCKS = N // BLOCK
-BLOCKS_PER_PIECE = PIECE // BLOCK
+NJ = PIECE // BLOCK
+NC = BLOCK // L
+TILE = P // NJ
+DIAG = NJ * TILE + NC
 LN_EPS = 1e-5
 
 FLOPS = 2 * P * P * B + 2 * P * N + 2 * P * N
+
+
+def own_columns(padded):
+    by_piece = padded.rearrange("p (i s) -> p i s", s=DIAG)[:, :, : NJ * TILE]
+    return by_piece.rearrange("p i (j r) -> p i j r", r=TILE)[:, :, :, :NC]
 
 
 def tile_scaleddpattention_kernel(tc, tab, mask, wdec, offs, out):
@@ -36,105 +42,106 @@ def tile_scaleddpattention_kernel(tc, tab, mask, wdec, offs, out):
         nc.sync.dma_start(offsets[:], offs)
 
         mask_row = mask.rearrange("o n -> (o n)")
-        mask_bc = [held.tile([P, PIECE], F32, name=f"mask_bc{i}") for i in range(N_PIECES)]
+        mask_bc = [held.tile([P, PIECE], F32, name=f"mask_bc{i}") for i in range(NI)]
         table = {}
         for name in ("v", "k", "q"):
             table[name] = held.tile([P, S], F32, name=f"table_{name}")
 
         def load_mask_piece(i):
-            queue = nc.sync if i % 2 == 0 else nc.scalar
-            queue.dma_start(mask_bc[i][:], mask_row[i * PIECE : (i + 1) * PIECE].partition_broadcast(P))
+            nc.sync.dma_start(mask_bc[i][:], mask_row[i * PIECE : (i + 1) * PIECE].partition_broadcast(P))
 
         def load_table(name, first_row):
             half = S // 2
             nc.sync.dma_start(table[name][:, :half], tab[first_row : first_row + P, :half])
-            nc.scalar.dma_start(table[name][:, half:], tab[first_row : first_row + P, half:])
+            nc.sync.dma_start(table[name][:, half:], tab[first_row : first_row + P, half:])
 
         load_mask_piece(0)
         load_table("k", P)
-        for i in range(1, N_PIECES):
+        for i in range(1, NI):
             load_mask_piece(i)
-        mask_seq = held.tile([B, L], F32, name="mask_seq")
-        nc.scalar.dma_start(mask_seq[:], mask.rearrange("o (b t) -> (o b) t", t=L))
+        mask_by_seq = held.tile([B, L], F32, name="mask_by_seq")
+        nc.gpsimd.dma_start(mask_by_seq[:], mask.rearrange("o (b t) -> (o b) t", t=L))
         load_table("q", 2 * P)
         load_table("v", 0)
         wdec_sb = held.tile([P, P], BF16, name="wdec_sb")
-        nc.scalar.dma_start(wdec_sb[:], wdec)
+        nc.gpsimd.dma_start(wdec_sb[:], wdec)
 
         ident = held.tile([P, P], F32, name="ident")
         make_identity(nc, ident[:])
         ident_bf = held.tile([P, P], BF16, name="ident_bf")
         nc.vector.tensor_copy(ident_bf[:], ident[:])
-        quarter = held.tile([P, SEQ_PER_BLOCK], F32, name="quarter")
-        nc.vector.reduce_sum(out=quarter[:], in_=ident[:].rearrange("p (c t) -> p c t", t=L), axis=AX.X)
-        nc.vector.tensor_scalar_mul(quarter[:], quarter[:], 1.0 / math.sqrt(P))
-        place = held.tile([P, L], F32, name="place")
-        nc.vector.reduce_sum(out=place[:], in_=ident[:].rearrange("p (c t) -> p t c", t=L), axis=AX.X)
-        slot = held.tile([B, SEQ_PER_BLOCK], F32, name="slot")
-        nc.vector.reduce_sum(
-            out=slot[:], in_=ident[:].rearrange("p (k c) -> p c k", c=SEQ_PER_BLOCK), axis=AX.X
+        to_row = held.tile([B, B], F32, name="to_row")
+        nc.vector.tensor_copy(
+            to_row[:].rearrange("b (j i c) -> b i j c", i=NI, c=NC),
+            ident[:].rearrange("b (i j c) -> b i j c", j=NJ, c=NC),
         )
-        slot_wide = slot[:].unsqueeze(2).to_broadcast([B, SEQ_PER_BLOCK, L])
+        slot = held.tile([B, NC], F32, name="slot")
+        nc.vector.reduce_sum(out=slot[:], in_=ident[:].rearrange("p (k c) -> p c k", c=NC), axis=AX.X)
+        slot_wide = slot[:].unsqueeze(2).to_broadcast([B, NC, L])
+        slot_scaled = held.tile([B, NC], F32, name="slot_scaled")
+        nc.vector.tensor_scalar_mul(slot_scaled[:], slot[:], 1.0 / math.sqrt(P))
         minus_half = held.tile([B, 1], F32, name="minus_half")
         nc.vector.memset(minus_half[:], -0.5)
-        DIAG = P + SEQ_PER_BLOCK
-        weights = held.tile([P, N_BLOCKS * DIAG], F32, name="weights")
-        nc.gpsimd.memset(weights[:], 0.0)
+        ksum_padded = held.tile([P, NI * DIAG], F32, name="ksum_padded")
+        nc.gpsimd.memset(ksum_padded[:], 0.0)
+        pool_padded = held.tile([P, NI * DIAG], F32, name="pool_padded")
+        nc.gpsimd.memset(pool_padded[:], 0.0)
 
+        mask_seq_ps = psum_held.tile([B, L], F32, name="mask_seq_ps")
+        nc.tensor.matmul(mask_seq_ps[:], lhsT=to_row[:], rhs=mask_by_seq[:], start=True, stop=True)
+        mask_seq = held.tile([B, L], F32, name="mask_seq")
+        nc.vector.tensor_copy(mask_seq[:], mask_seq_ps[:])
         mask_sum = held.tile([B, 1], F32, name="mask_sum")
         nc.vector.reduce_sum(out=mask_sum[:], in_=mask_seq[:], axis=AX.X)
         mean_weight = held.tile([B, 1], F32, name="mean_weight")
         nc.vector.reciprocal(mean_weight[:], mask_sum[:])
-        mask_wide = held.tile([B, SEQ_PER_BLOCK, L], F32, name="mask_wide")
-        nc.vector.tensor_tensor(
-            mask_wide[:], mask_seq[:].unsqueeze(1).to_broadcast([B, SEQ_PER_BLOCK, L]), slot_wide, ALU.mult
-        )
-        mean_wide = held.tile([B, SEQ_PER_BLOCK, L], F32, name="mean_wide")
+        mask_wide = held.tile([B, NC, L], F32, name="mask_wide")
+        nc.vector.tensor_tensor(mask_wide[:], mask_seq[:].unsqueeze(1).to_broadcast([B, NC, L]), slot_wide, ALU.mult)
+        mean_wide = held.tile([B, NC, L], F32, name="mean_wide")
         nc.vector.tensor_scalar_mul(mean_wide[:], slot_wide, mean_weight[:])
 
-        def look_up(name, i):
-            e = ring.tile([P, PIECE], F32, name=f"e_{name}")
+        def look_up(name, i, bufs):
+            e = ring.tile([P, PIECE], F32, name=f"e_{name}", bufs=bufs)
             picked = table[name][:].indirect(offsets[:, i * PIECE // 16 : (i + 1) * PIECE // 16])
             nc.vector.tensor_tensor(e[:], picked, mask_bc[i][:], ALU.mult)
             return e
 
-        ksum = held.tile([P, B], F32, name="ksum")
-        seq_per_piece = PIECE // L
-        for i in range(N_PIECES):
-            k = look_up("k", i)
-            nc.vector.reduce_sum(
-                out=ksum[:, i * seq_per_piece : (i + 1) * seq_per_piece],
-                in_=k[:].rearrange("d (b t) -> d b t", t=L),
-                axis=AX.X,
-            )
+        for i in range(NI):
+            k = look_up("k", i, NI)
+            for jc in range(NJ * NC):
+                j, c = divmod(jc, NC)
+                at = i * DIAG + j * TILE + c
+                seq = k[:, jc * L : (jc + 1) * L]
+                nc.scalar.activation(out=seq, in_=seq, func=ACT.Copy, accum_out=ksum_padded[:, at : at + 1])
 
-        cross_ps = psum_held.tile([P, B], F32, name="cross_ps")
-        for i in range(N_PIECES):
-            q = look_up("q", i)
-            for j in range(BLOCKS_PER_PIECE):
-                block = i * BLOCKS_PER_PIECE + j
-                own = slice(block * SEQ_PER_BLOCK, (block + 1) * SEQ_PER_BLOCK)
+        cross_ps = psum_held.tile([B, BLOCK], F32, name="cross_ps")
+        for i in range(NI):
+            q = look_up("q", i, 3)
+            for j in range(NJ):
+                block = i * NJ + j
                 nc.tensor.matmul(
-                    cross_ps[:, own], lhsT=q[:, j * BLOCK : (j + 1) * BLOCK], rhs=ksum[:, own], start=True, stop=True
+                    cross_ps[j * TILE : (j + 1) * TILE, :],
+                    lhsT=ksum_padded[:, block * TILE : (block + 1) * TILE],
+                    rhs=q[:, j * BLOCK : (j + 1) * BLOCK],
+                    start=(i == 0),
+                    stop=(i == NI - 1),
                 )
 
-        own_score = held.tile([P, B], F32, name="own_score")
+        own = held.tile([B, NC, L], F32, name="own")
         nc.vector.tensor_tensor(
-            own_score[:].rearrange("p (k c) -> p k c", c=SEQ_PER_BLOCK),
-            cross_ps[:].rearrange("p (k c) -> p k c", c=SEQ_PER_BLOCK),
-            quarter[:].unsqueeze(1).to_broadcast([P, N_BLOCKS, SEQ_PER_BLOCK]),
+            own[:],
+            cross_ps[:].rearrange("r (c t) -> r c t", t=L),
+            slot_scaled[:].unsqueeze(2).to_broadcast([B, NC, L]),
             ALU.mult,
         )
-        s_ps = psum_held.tile([B, L], F32, name="s_ps")
-        nc.tensor.matmul(s_ps[:], lhsT=own_score[:], rhs=place[:], start=True, stop=True)
+        score = held.tile([B, L], F32, name="score")
+        nc.vector.reduce_sum(out=score[:], in_=own[:].rearrange("r c t -> r t c"), axis=AX.X)
         neg_max = held.tile([B, 1], F32, name="neg_max")
-        nc.vector.reduce_max(out=neg_max[:], in_=s_ps[:], axis=AX.X, negate=True)
+        nc.vector.reduce_max(out=neg_max[:], in_=score[:], axis=AX.X, negate=True)
         expd = held.tile([B, L], F32, name="expd")
-        nc.scalar.activation(out=expd[:], in_=s_ps[:], func=ACT.Exp, bias=neg_max[:], scale=1.0)
-        y_wide = held.tile([B, SEQ_PER_BLOCK, L], F32, name="y_wide")
-        nc.vector.tensor_tensor(
-            y_wide[:], expd[:].unsqueeze(1).to_broadcast([B, SEQ_PER_BLOCK, L]), mask_wide[:], ALU.mult
-        )
+        nc.scalar.activation(out=expd[:], in_=score[:], func=ACT.Exp, bias=neg_max[:], scale=1.0)
+        y_wide = held.tile([B, NC, L], F32, name="y_wide")
+        nc.vector.tensor_tensor(y_wide[:], expd[:].unsqueeze(1).to_broadcast([B, NC, L]), mask_wide[:], ALU.mult)
         y_sum = held.tile([B, 1], F32, name="y_sum")
         nc.vector.reduce_sum(out=y_sum[:], in_=y_wide[:].rearrange("b c t -> b (c t)"), axis=AX.X)
         y_scale = held.tile([B, 1], F32, name="y_scale")
@@ -150,27 +157,24 @@ def tile_scaleddpattention_kernel(tc, tab, mask, wdec, offs, out):
         )
         pool_ps = psum_held.tile([P, B], F32, name="pool_ps")
         nc.tensor.transpose(pool_ps[:], pool_wide[:], ident[:])
-        nc.scalar.copy(
-            weights[:].rearrange("p (k s) -> p k s", s=DIAG)[:, :, :SEQ_PER_BLOCK],
-            pool_ps[:].rearrange("p (k c) -> p k c", c=SEQ_PER_BLOCK),
-        )
+        nc.scalar.copy(own_columns(pool_padded[:]), pool_ps[:].rearrange("p (j i c) -> p i j c", i=NI, c=NC))
 
         h_ps = psum_held.tile([B, P], F32, name="h_ps")
-        for i in range(N_PIECES):
-            v = look_up("v", i)
+        for i in range(NI):
+            v = look_up("v", i, 3)
             vT_ps = psum_ring.tile([P, PIECE], F32, name="vT_ps")
-            for j in range(BLOCKS_PER_PIECE):
+            for j in range(NJ):
                 nc.tensor.transpose(vT_ps[:, j * P : (j + 1) * P], v[:, j * BLOCK : (j + 1) * BLOCK], ident[:])
             vT = ring.tile([P, PIECE], F32, name="vT")
             nc.scalar.copy(vT[:], vT_ps[:])
-            for j in range(BLOCKS_PER_PIECE):
-                block = i * BLOCKS_PER_PIECE + j
+            for j in range(NJ):
+                block = i * NJ + j
                 nc.tensor.matmul(
-                    h_ps[:],
-                    lhsT=weights[:, block * P : (block + 1) * P],
+                    h_ps[j * TILE : (j + 1) * TILE, :],
+                    lhsT=pool_padded[:, block * TILE : (block + 1) * TILE],
                     rhs=vT[:, j * P : (j + 1) * P],
-                    start=(block == 0),
-                    stop=(block == N_BLOCKS - 1),
+                    start=(i == 0),
+                    stop=(i == NI - 1),
                 )
 
         stats = held.tile([B, 6], F32, name="stats")
@@ -190,5 +194,8 @@ def tile_scaleddpattention_kernel(tc, tab, mask, wdec, offs, out):
         out_ps = psum_held.tile([P, B], F32, name="out_ps")
         nc.tensor.matmul(out_ps[:], lhsT=wdec_sb[:], rhs=z[:], start=True, stop=True)
         out_sb = held.tile([P, B], F32, name="out_sb")
-        nc.vector.tensor_copy(out_sb[:], out_ps[:])
+        nc.vector.tensor_copy(
+            out_sb[:].rearrange("m (i j c) -> m i j c", j=NJ, c=NC),
+            out_ps[:].rearrange("m (j i c) -> m i j c", i=NI, c=NC),
+        )
         nc.sync.dma_start(out, out_sb[:])

@@ -20,6 +20,8 @@ NJ = PIECE // BLOCK
 NC = BLOCK // L
 TILE = P // NJ
 DIAG = NJ * TILE + NC
+BATCH = NI // 2
+SCALAR_PIECES = 6
 LN_EPS = 1e-5
 
 FLOPS = 2 * P * P * B + 2 * P * N + 2 * P * N
@@ -106,13 +108,23 @@ def tile_scaleddpattention_kernel(tc, tab, mask, wdec, offs, out):
             nc.vector.tensor_tensor(e[:], picked, mask_bc[i][:], ALU.mult)
             return e
 
+        left_to_vector = []
         for i in range(NI):
             k = look_up("k", i, NI)
+            if i >= SCALAR_PIECES:
+                left_to_vector.append((i, k))
+                continue
             for jc in range(NJ * NC):
                 j, c = divmod(jc, NC)
                 at = i * DIAG + j * TILE + c
                 seq = k[:, jc * L : (jc + 1) * L]
                 nc.scalar.activation(out=seq, in_=seq, func=ACT.Copy, accum_out=ksum_padded[:, at : at + 1])
+        for i, k in left_to_vector:
+            nc.vector.reduce_sum(
+                out=own_columns(ksum_padded[:])[:, i],
+                in_=k[:].rearrange("d (j c t) -> d j c t", c=NC, t=L),
+                axis=AX.X,
+            )
 
         cross_ps = psum_held.tile([B, BLOCK], F32, name="cross_ps")
         for i in range(NI):
@@ -127,46 +139,54 @@ def tile_scaleddpattention_kernel(tc, tab, mask, wdec, offs, out):
                     stop=(i == NI - 1),
                 )
 
-        own = held.tile([B, NC, L], F32, name="own")
-        nc.vector.tensor_tensor(
-            own[:],
-            cross_ps[:].rearrange("r (c t) -> r c t", t=L),
-            slot_scaled[:].unsqueeze(2).to_broadcast([B, NC, L]),
-            ALU.mult,
-        )
-        score = held.tile([B, L], F32, name="score")
-        nc.vector.reduce_sum(out=score[:], in_=own[:].rearrange("r c t -> r t c"), axis=AX.X)
-        neg_max = held.tile([B, 1], F32, name="neg_max")
-        nc.vector.reduce_max(out=neg_max[:], in_=score[:], axis=AX.X, negate=True)
         expd = held.tile([B, L], F32, name="expd")
-        nc.scalar.activation(out=expd[:], in_=score[:], func=ACT.Exp, bias=neg_max[:], scale=1.0)
-        y_wide = held.tile([B, NC, L], F32, name="y_wide")
-        nc.vector.tensor_tensor(y_wide[:], expd[:].unsqueeze(1).to_broadcast([B, NC, L]), mask_wide[:], ALU.mult)
-        y_sum = held.tile([B, 1], F32, name="y_sum")
-        nc.vector.reduce_sum(out=y_sum[:], in_=y_wide[:].rearrange("b c t -> b (c t)"), axis=AX.X)
-        y_scale = held.tile([B, 1], F32, name="y_scale")
-        nc.vector.reciprocal(y_scale[:], y_sum[:])
-        pool_wide = held.tile([B, P], F32, name="pool_wide")
-        nc.vector.scalar_tensor_tensor(
-            out=pool_wide[:],
-            in0=y_wide[:].rearrange("b c t -> b (c t)"),
-            scalar=y_scale[:],
-            in1=mean_wide[:].rearrange("b c t -> b (c t)"),
-            op0=ALU.mult,
-            op1=ALU.add,
-        )
-        pool_ps = psum_held.tile([P, B], F32, name="pool_ps")
-        nc.tensor.transpose(pool_ps[:], pool_wide[:], ident[:])
-        nc.scalar.copy(own_columns(pool_padded[:]), pool_ps[:].rearrange("p (j i c) -> p i j c", i=NI, c=NC))
+
+        def scores_to_exp():
+            own = held.tile([B, NC, L], F32, name="own")
+            nc.vector.tensor_tensor(
+                own[:],
+                cross_ps[:].rearrange("r (c t) -> r c t", t=L),
+                slot_scaled[:].unsqueeze(2).to_broadcast([B, NC, L]),
+                ALU.mult,
+            )
+            score = held.tile([B, L], F32, name="score")
+            nc.vector.reduce_sum(out=score[:], in_=own[:].rearrange("r c t -> r t c"), axis=AX.X)
+            neg_max = held.tile([B, 1], F32, name="neg_max")
+            nc.vector.reduce_max(out=neg_max[:], in_=score[:], axis=AX.X, negate=True)
+            nc.scalar.activation(out=expd[:], in_=score[:], func=ACT.Exp, bias=neg_max[:], scale=1.0)
+
+        def exp_to_weights():
+            y_wide = held.tile([B, NC, L], F32, name="y_wide")
+            nc.vector.tensor_tensor(y_wide[:], expd[:].unsqueeze(1).to_broadcast([B, NC, L]), mask_wide[:], ALU.mult)
+            y_sum = held.tile([B, 1], F32, name="y_sum")
+            nc.vector.reduce_sum(out=y_sum[:], in_=y_wide[:].rearrange("b c t -> b (c t)"), axis=AX.X)
+            y_scale = held.tile([B, 1], F32, name="y_scale")
+            nc.vector.reciprocal(y_scale[:], y_sum[:])
+            pool_wide = held.tile([B, P], F32, name="pool_wide")
+            nc.vector.scalar_tensor_tensor(
+                out=pool_wide[:],
+                in0=y_wide[:].rearrange("b c t -> b (c t)"),
+                scalar=y_scale[:],
+                in1=mean_wide[:].rearrange("b c t -> b (c t)"),
+                op0=ALU.mult,
+                op1=ALU.add,
+            )
+            pool_ps = psum_held.tile([P, B], F32, name="pool_ps")
+            nc.tensor.transpose(pool_ps[:], pool_wide[:], ident[:])
+            nc.scalar.copy(own_columns(pool_padded[:]), pool_ps[:].rearrange("p (j i c) -> p i j c", i=NI, c=NC))
 
         h_ps = psum_held.tile([B, P], F32, name="h_ps")
-        for i in range(NI):
-            v = look_up("v", i, 3)
+
+        def flipped_values(i):
+            v = look_up("v", i, BATCH)
             vT_ps = psum_ring.tile([P, PIECE], F32, name="vT_ps")
             for j in range(NJ):
                 nc.tensor.transpose(vT_ps[:, j * P : (j + 1) * P], v[:, j * BLOCK : (j + 1) * BLOCK], ident[:])
-            vT = ring.tile([P, PIECE], F32, name="vT")
+            vT = ring.tile([P, PIECE], F32, name="vT", bufs=BATCH + 2)
             nc.scalar.copy(vT[:], vT_ps[:])
+            return vT
+
+        def pool_values(i, vT):
             for j in range(NJ):
                 block = i * NJ + j
                 nc.tensor.matmul(
@@ -176,6 +196,17 @@ def tile_scaleddpattention_kernel(tc, tab, mask, wdec, offs, out):
                     start=(i == 0),
                     stop=(i == NI - 1),
                 )
+
+        flipped = []
+        for i in range(NI):
+            flipped.append(flipped_values(i))
+            if i == 1:
+                scores_to_exp()
+            if i == 2:
+                exp_to_weights()
+            if (i + 1) % BATCH == 0:
+                for done in range(i + 1 - BATCH, i + 1):
+                    pool_values(done, flipped[done])
 
         stats = held.tile([B, 6], F32, name="stats")
         nc.vector.bn_stats(stats[:], h_ps[:])

@@ -21,7 +21,7 @@ NC = BLOCK // L
 TILE = P // NJ
 DIAG = NJ * TILE + NC
 BATCH = NI // 2
-SCALAR_PIECES = 6
+SCALAR_PIECES = 7
 LN_EPS = 1e-5
 
 FLOPS = 2 * P * P * B + 2 * P * N + 2 * P * N
@@ -82,8 +82,8 @@ def tile_scaleddpattention_kernel(tc, tab, mask, wdec, offs, out):
         slot_wide = slot[:].unsqueeze(2).to_broadcast([B, NC, L])
         slot_scaled = held.tile([B, NC], F32, name="slot_scaled")
         nc.vector.tensor_scalar_mul(slot_scaled[:], slot[:], 1.0 / math.sqrt(P))
-        minus_half = held.tile([B, 1], F32, name="minus_half")
-        nc.vector.memset(minus_half[:], -0.5)
+        eps = held.tile([B, 1], F32, name="eps")
+        nc.vector.memset(eps[:], LN_EPS)
         ksum_padded = held.tile([P, NI * DIAG], F32, name="ksum_padded")
         nc.gpsimd.memset(ksum_padded[:], 0.0)
         pool_padded = held.tile([P, NI * DIAG], F32, name="pool_padded")
@@ -157,9 +157,16 @@ def tile_scaleddpattention_kernel(tc, tab, mask, wdec, offs, out):
 
         def exp_to_weights():
             y_wide = held.tile([B, NC, L], F32, name="y_wide")
-            nc.vector.tensor_tensor(y_wide[:], expd[:].unsqueeze(1).to_broadcast([B, NC, L]), mask_wide[:], ALU.mult)
             y_sum = held.tile([B, 1], F32, name="y_sum")
-            nc.vector.reduce_sum(out=y_sum[:], in_=y_wide[:].rearrange("b c t -> b (c t)"), axis=AX.X)
+            nc.vector.scalar_tensor_tensor(
+                out=y_wide[:],
+                in0=expd[:].unsqueeze(1).to_broadcast([B, NC, L]),
+                scalar=1.0,
+                in1=mask_wide[:],
+                op0=ALU.mult,
+                op1=ALU.mult,
+                accum_out=y_sum[:],
+            )
             y_scale = held.tile([B, 1], F32, name="y_scale")
             nc.vector.reciprocal(y_scale[:], y_sum[:])
             pool_wide = held.tile([B, P], F32, name="pool_wide")
@@ -200,9 +207,9 @@ def tile_scaleddpattention_kernel(tc, tab, mask, wdec, offs, out):
         flipped = []
         for i in range(NI):
             flipped.append(flipped_values(i))
-            if i == 1:
+            if i == 0:
                 scores_to_exp()
-            if i == 2:
+            if i == 1:
                 exp_to_weights()
             if (i + 1) % BATCH == 0:
                 for done in range(i + 1 - BATCH, i + 1):
@@ -212,10 +219,8 @@ def tile_scaleddpattention_kernel(tc, tab, mask, wdec, offs, out):
         nc.vector.bn_stats(stats[:], h_ps[:])
         mean_var = held.tile([B, 2], F32, name="mean_var")
         nc.vector.bn_aggr(mean_var[:], stats[:])
-        var_eps = held.tile([B, 1], F32, name="var_eps")
-        nc.vector.tensor_scalar_add(var_eps[:], mean_var[:, 1:2], LN_EPS)
         rstd = held.tile([B, 1], F32, name="rstd")
-        nc.gpsimd.tensor_tensor(rstd[:], var_eps[:], minus_half[:], ALU.pow)
+        nc.scalar.activation(out=rstd[:], in_=mean_var[:, 1:2], func=ACT.Abs_reciprocal_sqrt, bias=eps[:], scale=1.0)
         zT = held.tile([B, P], BF16, name="zT")
         nc.vector.tensor_scalar(zT[:], h_ps[:], mean_var[:, 0:1], rstd[:], op0=ALU.subtract, op1=ALU.mult)
         z_ps = psum_held.tile([P, B], BF16, name="z_ps")

@@ -21,8 +21,9 @@ NC = BLOCK // L
 TILE = P // NJ
 DIAG = NJ * TILE + NC
 BATCH = NI // 2
-SCALAR_PIECES = 7
+VECTOR_PIECE = NI - 2
 LN_EPS = 1e-5
+BIG = 1e30
 
 FLOPS = 2 * P * P * B + 2 * P * N + 2 * P * N
 
@@ -80,8 +81,8 @@ def tile_scaleddpattention_kernel(tc, tab, mask, wdec, offs, out):
         slot = held.tile([B, NC], F32, name="slot")
         nc.vector.reduce_sum(out=slot[:], in_=ident[:].rearrange("p (k c) -> p c k", c=NC), axis=AX.X)
         slot_wide = slot[:].unsqueeze(2).to_broadcast([B, NC, L])
-        slot_scaled = held.tile([B, NC], F32, name="slot_scaled")
-        nc.vector.tensor_scalar_mul(slot_scaled[:], slot[:], 1.0 / math.sqrt(P))
+        foreign = held.tile([B, NC, L], F32, name="foreign")
+        nc.vector.tensor_scalar(foreign[:], slot_wide, 1.0, BIG, op0=ALU.subtract, op1=ALU.mult)
         eps = held.tile([B, 1], F32, name="eps")
         nc.vector.memset(eps[:], LN_EPS)
         ksum_padded = held.tile([P, NI * DIAG], F32, name="ksum_padded")
@@ -108,23 +109,22 @@ def tile_scaleddpattention_kernel(tc, tab, mask, wdec, offs, out):
             nc.vector.tensor_tensor(e[:], picked, mask_bc[i][:], ALU.mult)
             return e
 
-        left_to_vector = []
+        k_pieces = []
         for i in range(NI):
             k = look_up("k", i, NI)
-            if i >= SCALAR_PIECES:
-                left_to_vector.append((i, k))
+            k_pieces.append(k)
+            if i == VECTOR_PIECE:
                 continue
             for jc in range(NJ * NC):
                 j, c = divmod(jc, NC)
                 at = i * DIAG + j * TILE + c
                 seq = k[:, jc * L : (jc + 1) * L]
                 nc.scalar.activation(out=seq, in_=seq, func=ACT.Copy, accum_out=ksum_padded[:, at : at + 1])
-        for i, k in left_to_vector:
-            nc.vector.reduce_sum(
-                out=own_columns(ksum_padded[:])[:, i],
-                in_=k[:].rearrange("d (j c t) -> d j c t", c=NC, t=L),
-                axis=AX.X,
-            )
+        nc.vector.reduce_sum(
+            out=own_columns(ksum_padded[:])[:, VECTOR_PIECE],
+            in_=k_pieces[VECTOR_PIECE][:].rearrange("d (j c t) -> d j c t", c=NC, t=L),
+            axis=AX.X,
+        )
 
         cross_ps = psum_held.tile([B, BLOCK], F32, name="cross_ps")
         for i in range(NI):
@@ -139,30 +139,30 @@ def tile_scaleddpattention_kernel(tc, tab, mask, wdec, offs, out):
                     stop=(i == NI - 1),
                 )
 
-        expd = held.tile([B, L], F32, name="expd")
+        expd = held.tile([B, BLOCK], F32, name="expd")
 
         def scores_to_exp():
-            own = held.tile([B, NC, L], F32, name="own")
-            nc.vector.tensor_tensor(
-                own[:],
-                cross_ps[:].rearrange("r (c t) -> r c t", t=L),
-                slot_scaled[:].unsqueeze(2).to_broadcast([B, NC, L]),
-                ALU.mult,
+            score = held.tile([B, BLOCK], F32, name="score")
+            nc.vector.scalar_tensor_tensor(
+                out=score[:],
+                in0=cross_ps[:],
+                scalar=1.0 / math.sqrt(P),
+                in1=foreign[:].rearrange("r c t -> r (c t)"),
+                op0=ALU.mult,
+                op1=ALU.add,
             )
-            score = held.tile([B, L], F32, name="score")
-            nc.vector.reduce_sum(out=score[:], in_=own[:].rearrange("r c t -> r t c"), axis=AX.X)
             neg_max = held.tile([B, 1], F32, name="neg_max")
             nc.vector.reduce_max(out=neg_max[:], in_=score[:], axis=AX.X, negate=True)
             nc.scalar.activation(out=expd[:], in_=score[:], func=ACT.Exp, bias=neg_max[:], scale=1.0)
 
         def exp_to_weights():
-            y_wide = held.tile([B, NC, L], F32, name="y_wide")
+            y_wide = held.tile([B, BLOCK], F32, name="y_wide")
             y_sum = held.tile([B, 1], F32, name="y_sum")
             nc.vector.scalar_tensor_tensor(
                 out=y_wide[:],
-                in0=expd[:].unsqueeze(1).to_broadcast([B, NC, L]),
+                in0=expd[:],
                 scalar=1.0,
-                in1=mask_wide[:],
+                in1=mask_wide[:].rearrange("r c t -> r (c t)"),
                 op0=ALU.mult,
                 op1=ALU.mult,
                 accum_out=y_sum[:],
@@ -172,7 +172,7 @@ def tile_scaleddpattention_kernel(tc, tab, mask, wdec, offs, out):
             pool_wide = held.tile([B, P], F32, name="pool_wide")
             nc.vector.scalar_tensor_tensor(
                 out=pool_wide[:],
-                in0=y_wide[:].rearrange("b c t -> b (c t)"),
+                in0=y_wide[:],
                 scalar=y_scale[:],
                 in1=mean_wide[:].rearrange("b c t -> b (c t)"),
                 op0=ALU.mult,

@@ -58,16 +58,17 @@ def tile_scaleddpattention_kernel(tc, tab, mask, wdec, offs, out):
             nc.sync.dma_start(table[name][:, :half], tab[first_row : first_row + P, :half])
             nc.sync.dma_start(table[name][:, half:], tab[first_row : first_row + P, half:])
 
-        load_mask_piece(0)
+        mask_by_seq = held.tile([B, L], F32, name="mask_by_seq")
+        nc.sync.dma_start(mask_by_seq[:], mask.rearrange("o (b t) -> (o b) t", t=L))
+        mask_first = held.tile([TILE, PIECE], F32, name="mask_first")
+        nc.sync.dma_start(mask_first[:], mask_row[:PIECE].partition_broadcast(TILE))
         load_table("k", P)
         for i in range(1, NI):
             load_mask_piece(i)
-        mask_by_seq = held.tile([B, L], F32, name="mask_by_seq")
-        nc.gpsimd.dma_start(mask_by_seq[:], mask.rearrange("o (b t) -> (o b) t", t=L))
         load_table("q", 2 * P)
         load_table("v", 0)
         wdec_sb = held.tile([P, P], BF16, name="wdec_sb")
-        nc.gpsimd.dma_start(wdec_sb[:], wdec)
+        nc.sync.dma_start(wdec_sb[:], wdec)
 
         ident = held.tile([P, P], F32, name="ident")
         make_identity(nc, ident[:])
@@ -83,6 +84,8 @@ def tile_scaleddpattention_kernel(tc, tab, mask, wdec, offs, out):
         slot_wide = slot[:].unsqueeze(2).to_broadcast([B, NC, L])
         foreign = held.tile([B, NC, L], F32, name="foreign")
         nc.vector.tensor_scalar(foreign[:], slot_wide, 1.0, BIG, op0=ALU.subtract, op1=ALU.mult)
+        first_row = held.tile([TILE, P], F32, name="first_row")
+        nc.vector.tensor_copy(first_row[:], ident[:TILE, 0:1].to_broadcast([TILE, P]))
         eps = held.tile([B, 1], F32, name="eps")
         nc.vector.memset(eps[:], LN_EPS)
         ksum_padded = held.tile([P, NI * DIAG], F32, name="ksum_padded")
@@ -102,6 +105,10 @@ def tile_scaleddpattention_kernel(tc, tab, mask, wdec, offs, out):
         nc.vector.tensor_tensor(mask_wide[:], mask_seq[:].unsqueeze(1).to_broadcast([B, NC, L]), slot_wide, ALU.mult)
         mean_wide = held.tile([B, NC, L], F32, name="mean_wide")
         nc.vector.tensor_scalar_mul(mean_wide[:], slot_wide, mean_weight[:])
+
+        spread_ps = psum_ring.tile([P, PIECE], F32, name="spread_ps", tag="bank")
+        nc.tensor.matmul(spread_ps[:], lhsT=first_row[:], rhs=mask_first[:], start=True, stop=True)
+        nc.vector.tensor_copy(mask_bc[0][:], spread_ps[:])
 
         def look_up(name, i, bufs):
             e = ring.tile([P, PIECE], F32, name=f"e_{name}", bufs=bufs)
@@ -186,7 +193,7 @@ def tile_scaleddpattention_kernel(tc, tab, mask, wdec, offs, out):
 
         def flipped_values(i):
             v = look_up("v", i, BATCH)
-            vT_ps = psum_ring.tile([P, PIECE], F32, name="vT_ps")
+            vT_ps = psum_ring.tile([P, PIECE], F32, name="vT_ps", tag="bank")
             for j in range(NJ):
                 nc.tensor.transpose(vT_ps[:, j * P : (j + 1) * P], v[:, j * BLOCK : (j + 1) * BLOCK], ident[:])
             vT = ring.tile([P, PIECE], F32, name="vT", bufs=BATCH + 2)

@@ -21,6 +21,7 @@ NC = BLOCK // L
 TILE = P // NJ
 DIAG = NJ * TILE + NC
 BATCH = NI // 2
+PLACES = 3
 VECTOR_PIECE = NI - 2
 LN_EPS = 1e-5
 BIG = 1e30
@@ -39,7 +40,6 @@ def tile_scaleddpattention_kernel(tc, tab, mask, wdec, offs, out):
         tc.tile_pool(name="held", bufs=1) as held,
         tc.tile_pool(name="ring", bufs=3) as ring,
         tc.psum_pool(name="psum_held", bufs=1) as psum_held,
-        tc.psum_pool(name="psum_ring", bufs=2) as psum_ring,
     ):
         offsets = held.tile([P, N // 16], U16, name="offsets")
         nc.sync.dma_start(offsets[:], offs)
@@ -82,7 +82,7 @@ def tile_scaleddpattention_kernel(tc, tab, mask, wdec, offs, out):
         slot = held.tile([B, NC], F32, name="slot")
         nc.vector.reduce_sum(out=slot[:], in_=ident[:].rearrange("p (k c) -> p c k", c=NC), axis=AX.X)
         slot_wide = slot[:].unsqueeze(2).to_broadcast([B, NC, L])
-        foreign = held.tile([B, NC, L], F32, name="foreign")
+        foreign = held.tile([B, NC, L], F32, name="foreign", tag="values_place0")
         nc.vector.tensor_scalar(foreign[:], slot_wide, 1.0, BIG, op0=ALU.subtract, op1=ALU.mult)
         first_row = held.tile([TILE, P], F32, name="first_row")
         nc.vector.tensor_copy(first_row[:], ident[:TILE, 0:1].to_broadcast([TILE, P]))
@@ -101,20 +101,22 @@ def tile_scaleddpattention_kernel(tc, tab, mask, wdec, offs, out):
         nc.vector.reduce_sum(out=mask_sum[:], in_=mask_seq[:], axis=AX.X)
         mean_weight = held.tile([B, 1], F32, name="mean_weight")
         nc.vector.reciprocal(mean_weight[:], mask_sum[:])
-        mask_wide = held.tile([B, NC, L], F32, name="mask_wide")
+        mask_wide = held.tile([B, NC, L], F32, name="mask_wide", tag="values_place1")
         nc.vector.tensor_tensor(mask_wide[:], mask_seq[:].unsqueeze(1).to_broadcast([B, NC, L]), slot_wide, ALU.mult)
-        mean_wide = held.tile([B, NC, L], F32, name="mean_wide")
+        mean_wide = held.tile([B, NC, L], F32, name="mean_wide", tag="values_place2")
         nc.vector.tensor_scalar_mul(mean_wide[:], slot_wide, mean_weight[:])
 
-        spread_ps = psum_ring.tile([P, PIECE], F32, name="spread_ps", tag="bank")
+        spread_ps = psum_held.tile([P, PIECE], F32, name="spread_ps", tag="bank1")
         nc.tensor.matmul(spread_ps[:], lhsT=first_row[:], rhs=mask_first[:], start=True, stop=True)
         nc.vector.tensor_copy(mask_bc[0][:], spread_ps[:])
 
-        def look_up(name, i, bufs):
-            e = ring.tile([P, PIECE], F32, name=f"e_{name}", bufs=bufs)
+        def look_up_into(e, name, i):
             picked = table[name][:].indirect(offsets[:, i * PIECE // 16 : (i + 1) * PIECE // 16])
             nc.vector.tensor_tensor(e[:], picked, mask_bc[i][:], ALU.mult)
             return e
+
+        def look_up(name, i, bufs):
+            return look_up_into(ring.tile([P, PIECE], F32, name=f"e_{name}", bufs=bufs), name, i)
 
         k_pieces = []
         for i in range(NI):
@@ -133,7 +135,7 @@ def tile_scaleddpattention_kernel(tc, tab, mask, wdec, offs, out):
             axis=AX.X,
         )
 
-        cross_ps = psum_held.tile([B, BLOCK], F32, name="cross_ps")
+        cross_ps = psum_held.tile([B, BLOCK], F32, name="cross_ps", tag="bank0")
         for i in range(NI):
             q = look_up("q", i, 3)
             for j in range(NJ):
@@ -192,8 +194,9 @@ def tile_scaleddpattention_kernel(tc, tab, mask, wdec, offs, out):
         h_ps = psum_held.tile([B, P], F32, name="h_ps")
 
         def flipped_values(i):
-            v = look_up("v", i, BATCH)
-            vT_ps = psum_ring.tile([P, PIECE], F32, name="vT_ps", tag="bank")
+            place = "values_first" if i == 0 else f"values_place{(i - 1) % PLACES}"
+            v = look_up_into(held.tile([P, PIECE], F32, name="e_v", tag=place), "v", i)
+            vT_ps = psum_held.tile([P, PIECE], F32, name="vT_ps", tag=f"bank{i % 2}")
             for j in range(NJ):
                 nc.tensor.transpose(vT_ps[:, j * P : (j + 1) * P], v[:, j * BLOCK : (j + 1) * BLOCK], ident[:])
             vT = ring.tile([P, PIECE], F32, name="vT", bufs=BATCH + 2)

@@ -22,7 +22,6 @@ TILE = P // NJ
 DIAG = NJ * TILE + NC
 BATCH = NI // 2
 PLACES = 3
-VECTOR_PIECE = NI - 2
 LN_EPS = 1e-5
 BIG = 1e30
 
@@ -60,8 +59,7 @@ def tile_scaleddpattention_kernel(tc, tab, mask, wdec, offs, out):
 
         mask_by_seq = held.tile([B, L], F32, name="mask_by_seq")
         nc.sync.dma_start(mask_by_seq[:], mask.rearrange("o (b t) -> (o b) t", t=L))
-        mask_first = held.tile([TILE, PIECE], F32, name="mask_first")
-        nc.sync.dma_start(mask_first[:], mask_row[:PIECE].partition_broadcast(TILE))
+        load_mask_piece(0)
         load_table("k", P)
         for i in range(1, NI):
             load_mask_piece(i)
@@ -84,8 +82,6 @@ def tile_scaleddpattention_kernel(tc, tab, mask, wdec, offs, out):
         slot_wide = slot[:].unsqueeze(2).to_broadcast([B, NC, L])
         foreign = held.tile([B, NC, L], F32, name="foreign", tag="values_place0")
         nc.vector.tensor_scalar(foreign[:], slot_wide, 1.0, BIG, op0=ALU.subtract, op1=ALU.mult)
-        first_row = held.tile([TILE, P], F32, name="first_row")
-        nc.vector.tensor_copy(first_row[:], ident[:TILE, 0:1].to_broadcast([TILE, P]))
         eps = held.tile([B, 1], F32, name="eps")
         nc.vector.memset(eps[:], LN_EPS)
         ksum_padded = held.tile([P, NI * DIAG], F32, name="ksum_padded")
@@ -103,12 +99,8 @@ def tile_scaleddpattention_kernel(tc, tab, mask, wdec, offs, out):
         nc.vector.reciprocal(mean_weight[:], mask_sum[:])
         mask_wide = held.tile([B, NC, L], F32, name="mask_wide", tag="values_place1")
         nc.vector.tensor_tensor(mask_wide[:], mask_seq[:].unsqueeze(1).to_broadcast([B, NC, L]), slot_wide, ALU.mult)
-        mean_wide = held.tile([B, NC, L], F32, name="mean_wide", tag="values_place2")
+        mean_wide = ring.tile([B, NC, L], F32, name="mean_wide", tag="e_k", bufs=NI + 1)
         nc.vector.tensor_scalar_mul(mean_wide[:], slot_wide, mean_weight[:])
-
-        spread_ps = psum_held.tile([P, PIECE], F32, name="spread_ps", tag="bank1")
-        nc.tensor.matmul(spread_ps[:], lhsT=first_row[:], rhs=mask_first[:], start=True, stop=True)
-        nc.vector.tensor_copy(mask_bc[0][:], spread_ps[:])
 
         def look_up_into(e, name, i):
             picked = table[name][:].indirect(offsets[:, i * PIECE // 16 : (i + 1) * PIECE // 16])
@@ -118,22 +110,13 @@ def tile_scaleddpattention_kernel(tc, tab, mask, wdec, offs, out):
         def look_up(name, i, bufs):
             return look_up_into(ring.tile([P, PIECE], F32, name=f"e_{name}", bufs=bufs), name, i)
 
-        k_pieces = []
         for i in range(NI):
-            k = look_up("k", i, NI)
-            k_pieces.append(k)
-            if i == VECTOR_PIECE:
-                continue
+            k = look_up("k", i, NI + 1)
             for jc in range(NJ * NC):
                 j, c = divmod(jc, NC)
                 at = i * DIAG + j * TILE + c
                 seq = k[:, jc * L : (jc + 1) * L]
                 nc.scalar.activation(out=seq, in_=seq, func=ACT.Copy, accum_out=ksum_padded[:, at : at + 1])
-        nc.vector.reduce_sum(
-            out=own_columns(ksum_padded[:])[:, VECTOR_PIECE],
-            in_=k_pieces[VECTOR_PIECE][:].rearrange("d (j c t) -> d j c t", c=NC, t=L),
-            axis=AX.X,
-        )
 
         cross_ps = psum_held.tile([B, BLOCK], F32, name="cross_ps", tag="bank0")
         for i in range(NI):
@@ -148,7 +131,7 @@ def tile_scaleddpattention_kernel(tc, tab, mask, wdec, offs, out):
                     stop=(i == NI - 1),
                 )
 
-        expd = held.tile([B, BLOCK], F32, name="expd")
+        expd = held.tile([B, BLOCK], F32, name="expd", tag="values_place2")
 
         def scores_to_exp():
             score = held.tile([B, BLOCK], F32, name="score")

@@ -183,7 +183,10 @@ def tile_scaleddpattention_kernel(tc, tab, mask, wdec, offs, out):
             for j in range(NJ):
                 nc.tensor.transpose(vT_ps[:, j * P : (j + 1) * P], v[:, j * BLOCK : (j + 1) * BLOCK], ident[:])
             vT = ring.tile([P, PIECE], F32, name="vT", bufs=BATCH + 2)
-            nc.scalar.copy(vT[:], vT_ps[:])
+            if i == NI - 1:
+                nc.vector.tensor_copy(vT[:], vT_ps[:])
+            else:
+                nc.scalar.copy(vT[:], vT_ps[:])
             return vT
 
         def pool_values(i, vT):

@@ -20,7 +20,7 @@ NJ = PIECE // BLOCK
 NC = BLOCK // L
 TILE = P // NJ
 DIAG = NJ * TILE + NC
-BATCH = NI // 2
+PART_BLOCKS = [3, 3, 4, 4, 4, 4, 4, 4, 2]
 PLACES = 3
 LN_EPS = 1e-5
 BIG = 1e30
@@ -44,13 +44,14 @@ def tile_scaleddpattention_kernel(tc, tab, mask, wdec, offs, out):
         nc.sync.dma_start(offsets[:], offs)
 
         mask_row = mask.rearrange("o n -> (o n)")
-        mask_bc = [held.tile([P, PIECE], F32, name=f"mask_bc{i}") for i in range(NI)]
+        mask_bc = held.tile([P, N], F32, name="mask_bc")
         table = {}
         for name in ("v", "k", "q"):
             table[name] = held.tile([P, S], F32, name=f"table_{name}")
 
         def load_mask_piece(i):
-            nc.sync.dma_start(mask_bc[i][:], mask_row[i * PIECE : (i + 1) * PIECE].partition_broadcast(P))
+            piece = slice(i * PIECE, (i + 1) * PIECE)
+            nc.sync.dma_start(mask_bc[:, piece], mask_row[piece].partition_broadcast(P))
 
         def load_table(name, first_row):
             half = S // 2
@@ -80,10 +81,8 @@ def tile_scaleddpattention_kernel(tc, tab, mask, wdec, offs, out):
         slot = held.tile([B, NC], F32, name="slot")
         nc.vector.reduce_sum(out=slot[:], in_=ident[:].rearrange("p (k c) -> p c k", c=NC), axis=AX.X)
         slot_wide = slot[:].unsqueeze(2).to_broadcast([B, NC, L])
-        foreign = held.tile([B, NC, L], F32, name="foreign", tag="values_place0")
+        foreign = held.tile([B, NC, L], F32, name="foreign")
         nc.vector.tensor_scalar(foreign[:], slot_wide, 1.0, BIG, op0=ALU.subtract, op1=ALU.mult)
-        eps = held.tile([B, 1], F32, name="eps")
-        nc.vector.memset(eps[:], LN_EPS)
         ksum_padded = held.tile([P, NI * DIAG], F32, name="ksum_padded")
         nc.gpsimd.memset(ksum_padded[:], 0.0)
         pool_padded = held.tile([P, NI * DIAG], F32, name="pool_padded")
@@ -91,24 +90,26 @@ def tile_scaleddpattention_kernel(tc, tab, mask, wdec, offs, out):
 
         mask_seq_ps = psum_held.tile([B, L], F32, name="mask_seq_ps")
         nc.tensor.matmul(mask_seq_ps[:], lhsT=to_row[:], rhs=mask_by_seq[:], start=True, stop=True)
-        mask_seq = held.tile([B, L], F32, name="mask_seq")
-        nc.vector.tensor_copy(mask_seq[:], mask_seq_ps[:])
-        mask_sum = held.tile([B, 1], F32, name="mask_sum")
-        nc.vector.reduce_sum(out=mask_sum[:], in_=mask_seq[:], axis=AX.X)
+        mask_and_sum = held.tile([B, L + 1], F32, name="mask_and_sum")
+        nc.vector.tensor_copy(mask_and_sum[:, :L], mask_seq_ps[:])
+        nc.vector.reduce_sum(out=mask_and_sum[:, L:], in_=mask_seq_ps[:], axis=AX.X)
+        logs = held.tile([B, L + 1], F32, name="logs")
+        nc.scalar.activation(out=logs[:], in_=mask_and_sum[:], func=ACT.Ln)
         mean_weight = held.tile([B, 1], F32, name="mean_weight")
-        nc.vector.reciprocal(mean_weight[:], mask_sum[:])
-        mask_wide = held.tile([B, NC, L], F32, name="mask_wide", tag="values_place1")
-        nc.vector.tensor_tensor(mask_wide[:], mask_seq[:].unsqueeze(1).to_broadcast([B, NC, L]), slot_wide, ALU.mult)
+        nc.scalar.activation(out=mean_weight[:], in_=logs[:, L:], func=ACT.Exp, scale=-1.0)
+        log_mask = held.tile([B, NC, L], F32, name="log_mask", tag="values_place0")
+        nc.vector.tensor_tensor(log_mask[:], foreign[:], logs[:, :L].unsqueeze(1).to_broadcast([B, NC, L]), ALU.add)
         mean_wide = ring.tile([B, NC, L], F32, name="mean_wide", tag="e_k", bufs=NI + 1)
         nc.vector.tensor_scalar_mul(mean_wide[:], slot_wide, mean_weight[:])
 
-        def look_up_into(e, name, i):
-            picked = table[name][:].indirect(offsets[:, i * PIECE // 16 : (i + 1) * PIECE // 16])
-            nc.vector.tensor_tensor(e[:], picked, mask_bc[i][:], ALU.mult)
+        def look_up_into(e, name, first):
+            end = first + e.shape[1]
+            picked = table[name][:].indirect(offsets[:, first // 16 : end // 16])
+            nc.vector.tensor_tensor(e[:], picked, mask_bc[:, first:end], ALU.mult)
             return e
 
         def look_up(name, i, bufs):
-            return look_up_into(ring.tile([P, PIECE], F32, name=f"e_{name}", bufs=bufs), name, i)
+            return look_up_into(ring.tile([P, PIECE], F32, name=f"e_{name}", bufs=bufs), name, i * PIECE)
 
         for i in range(NI):
             k = look_up("k", i, NI + 1)
@@ -131,7 +132,9 @@ def tile_scaleddpattention_kernel(tc, tab, mask, wdec, offs, out):
                     stop=(i == NI - 1),
                 )
 
-        expd = held.tile([B, BLOCK], F32, name="expd", tag="values_place2")
+        y = held.tile([B, BLOCK], F32, name="y", tag="values_place1")
+        y_sum = held.tile([B, 1], F32, name="y_sum")
+        eps_row = held.tile([B, 1], F32, name="eps_row")
 
         def scores_to_exp():
             score = held.tile([B, BLOCK], F32, name="score")
@@ -139,84 +142,80 @@ def tile_scaleddpattention_kernel(tc, tab, mask, wdec, offs, out):
                 out=score[:],
                 in0=cross_ps[:],
                 scalar=1.0 / math.sqrt(P),
-                in1=foreign[:].rearrange("r c t -> r (c t)"),
+                in1=log_mask[:].rearrange("r c t -> r (c t)"),
                 op0=ALU.mult,
                 op1=ALU.add,
             )
             neg_max = held.tile([B, 1], F32, name="neg_max")
             nc.vector.reduce_max(out=neg_max[:], in_=score[:], axis=AX.X, negate=True)
-            nc.scalar.activation(out=expd[:], in_=score[:], func=ACT.Exp, bias=neg_max[:], scale=1.0)
+            nc.scalar.activation(out=y[:], in_=score[:], func=ACT.Exp, bias=neg_max[:], scale=1.0, accum_out=y_sum[:])
 
         def exp_to_weights():
-            y_wide = held.tile([B, BLOCK], F32, name="y_wide")
-            y_sum = held.tile([B, 1], F32, name="y_sum")
-            nc.vector.scalar_tensor_tensor(
-                out=y_wide[:],
-                in0=expd[:],
-                scalar=1.0,
-                in1=mask_wide[:].rearrange("r c t -> r (c t)"),
-                op0=ALU.mult,
-                op1=ALU.mult,
-                accum_out=y_sum[:],
-            )
-            y_scale = held.tile([B, 1], F32, name="y_scale")
-            nc.vector.reciprocal(y_scale[:], y_sum[:])
-            pool_wide = held.tile([B, P], F32, name="pool_wide")
+            pool_wide = held.tile([B, P], F32, name="pool_wide", tag="values_place2")
             nc.vector.scalar_tensor_tensor(
                 out=pool_wide[:],
-                in0=y_wide[:],
-                scalar=y_scale[:],
-                in1=mean_wide[:].rearrange("b c t -> b (c t)"),
+                in0=mean_wide[:].rearrange("b c t -> b (c t)"),
+                scalar=y_sum[:],
+                in1=y[:],
                 op0=ALU.mult,
                 op1=ALU.add,
             )
-            pool_ps = psum_held.tile([P, B], F32, name="pool_ps")
+            pool_ps = psum_held.tile([P, B], F32, name="pool_ps", tag="bank1")
             nc.tensor.transpose(pool_ps[:], pool_wide[:], ident[:])
             nc.scalar.copy(own_columns(pool_padded[:]), pool_ps[:].rearrange("p (j i c) -> p i j c", i=NI, c=NC))
+            nc.scalar.activation(out=eps_row[:], in_=y_sum[:], func=ACT.Square, scale=math.sqrt(LN_EPS))
 
         h_ps = psum_held.tile([B, P], F32, name="h_ps")
 
-        def flipped_values(i):
-            place = "values_first" if i == 0 else f"values_place{(i - 1) % PLACES}"
-            v = look_up_into(held.tile([P, PIECE], F32, name="e_v", tag=place), "v", i)
-            vT_ps = psum_held.tile([P, PIECE], F32, name="vT_ps", tag=f"bank{i % 2}")
-            for j in range(NJ):
-                nc.tensor.transpose(vT_ps[:, j * P : (j + 1) * P], v[:, j * BLOCK : (j + 1) * BLOCK], ident[:])
-            vT = ring.tile([P, PIECE], F32, name="vT", bufs=BATCH + 2)
-            if i == NI - 1:
-                nc.vector.tensor_copy(vT[:], vT_ps[:])
-            else:
-                nc.scalar.copy(vT[:], vT_ps[:])
+        def look_up_values(part):
+            place = "values_first" if part == 0 else f"values_place{(part - 1) % PLACES}"
+            v = held.tile([P, PART_BLOCKS[part] * BLOCK], F32, name="e_v", tag=place)
+            return look_up_into(v, "v", sum(PART_BLOCKS[:part]) * BLOCK)
+
+        def flip(part, v):
+            vT_ps = psum_held.tile([P, PIECE], F32, name="vT_ps", tag=f"bank{part % 2}")
+            columns = PART_BLOCKS[part] * P
+            for at in range(0, columns, P):
+                nc.tensor.transpose(vT_ps[:, at : at + P], v[:, at : at + BLOCK], ident[:])
+            vT = ring.tile([P, PIECE], F32, name="vT", bufs=len(PART_BLOCKS))
+            copy = nc.vector.tensor_copy if part == len(PART_BLOCKS) - 1 else nc.scalar.copy
+            copy(vT[:, :columns], vT_ps[:, :columns])
             return vT
 
-        def pool_values(i, vT):
-            for j in range(NJ):
-                block = i * NJ + j
+        def pool_values(part, vT):
+            for n in range(PART_BLOCKS[part]):
+                block = sum(PART_BLOCKS[:part]) + n
+                i, j = divmod(block, NJ)
                 nc.tensor.matmul(
                     h_ps[j * TILE : (j + 1) * TILE, :],
                     lhsT=pool_padded[:, block * TILE : (block + 1) * TILE],
-                    rhs=vT[:, j * P : (j + 1) * P],
+                    rhs=vT[:, n * P : (n + 1) * P],
                     start=(i == 0),
                     stop=(i == NI - 1),
                 )
 
-        flipped = []
-        for i in range(NI):
-            flipped.append(flipped_values(i))
-            if i == 0:
-                scores_to_exp()
-            if i == 1:
-                exp_to_weights()
-            if (i + 1) % BATCH == 0:
-                for done in range(i + 1 - BATCH, i + 1):
-                    pool_values(done, flipped[done])
+        v0 = look_up_values(0)
+        scores_to_exp()
+        vT = [flip(0, v0)]
+        v1 = look_up_values(1)
+        exp_to_weights()
+        vT.append(flip(1, v1))
+        pool_values(0, vT[0])
+        vT.append(flip(2, look_up_values(2)))
+        pool_values(1, vT[1])
+        for part in range(3, len(PART_BLOCKS), 2):
+            vT.append(flip(part, look_up_values(part)))
+            vT.append(flip(part + 1, look_up_values(part + 1)))
+            pool_values(part - 1, vT[part - 1])
+            pool_values(part, vT[part])
+        pool_values(part + 1, vT[part + 1])
 
         stats = held.tile([B, 6], F32, name="stats")
         nc.vector.bn_stats(stats[:], h_ps[:])
         mean_var = held.tile([B, 2], F32, name="mean_var")
         nc.vector.bn_aggr(mean_var[:], stats[:])
         rstd = held.tile([B, 1], F32, name="rstd")
-        nc.scalar.activation(out=rstd[:], in_=mean_var[:, 1:2], func=ACT.Abs_reciprocal_sqrt, bias=eps[:], scale=1.0)
+        nc.scalar.activation(out=rstd[:], in_=mean_var[:, 1:2], func=ACT.Abs_reciprocal_sqrt, bias=eps_row[:], scale=1.0)
         zT = held.tile([B, P], BF16, name="zT")
         nc.vector.tensor_scalar(zT[:], h_ps[:], mean_var[:, 0:1], rstd[:], op0=ALU.subtract, op1=ALU.mult)
         z_ps = psum_held.tile([P, B], BF16, name="z_ps")

@@ -72,35 +72,48 @@ def tile_scaleddpattention_kernel(tc, tab, mask, wdec, offs, out):
         ident = held.tile([P, P], F32, name="ident")
         make_identity(nc, ident[:])
         ident_bf = held.tile([P, P], BF16, name="ident_bf")
-        nc.vector.tensor_copy(ident_bf[:], ident[:])
+        nc.scalar.copy(ident_bf[:], ident[:])
         to_row = held.tile([B, B], F32, name="to_row")
-        nc.vector.tensor_copy(
+        nc.scalar.copy(
             to_row[:].rearrange("b (j i c) -> b i j c", i=NI, c=NC),
             ident[:].rearrange("b (i j c) -> b i j c", j=NJ, c=NC),
         )
-        slot = held.tile([B, NC], F32, name="slot")
-        nc.vector.reduce_sum(out=slot[:], in_=ident[:].rearrange("p (k c) -> p c k", c=NC), axis=AX.X)
-        slot_wide = slot[:].unsqueeze(2).to_broadcast([B, NC, L])
-        foreign = held.tile([B, NC, L], F32, name="foreign")
-        nc.vector.tensor_scalar(foreign[:], slot_wide, 1.0, BIG, op0=ALU.subtract, op1=ALU.mult)
-        ksum_padded = held.tile([P, NI * DIAG], F32, name="ksum_padded")
-        nc.gpsimd.memset(ksum_padded[:], 0.0)
+        slot = held.tile([B, NC], F32, name="slot", tag="ksum_place")
+        every_nc = held.tile([B, B // NC], F32, name="every_nc")
+        for c in range(NC):
+            nc.scalar.activation(
+                out=every_nc[:],
+                in_=ident[:].rearrange("p (k c) -> p c k", c=NC)[:, c, :],
+                func=ACT.Copy,
+                accum_out=slot[:, c : c + 1],
+            )
+        foreign = held.tile([B, NC], F32, name="foreign")
+        nc.scalar.activation(out=foreign[:], in_=slot[:], func=ACT.Copy, scale=BIG, bias=-BIG)
         pool_padded = held.tile([P, NI * DIAG], F32, name="pool_padded")
-        nc.gpsimd.memset(pool_padded[:], 0.0)
+        nc.vector.memset(pool_padded[:], 0.0)
 
         mask_seq_ps = psum_held.tile([B, L], F32, name="mask_seq_ps")
         nc.tensor.matmul(mask_seq_ps[:], lhsT=to_row[:], rhs=mask_by_seq[:], start=True, stop=True)
         mask_and_sum = held.tile([B, L + 1], F32, name="mask_and_sum")
-        nc.vector.tensor_copy(mask_and_sum[:, :L], mask_seq_ps[:])
-        nc.vector.reduce_sum(out=mask_and_sum[:, L:], in_=mask_seq_ps[:], axis=AX.X)
+        nc.scalar.activation(
+            out=mask_and_sum[:, :L], in_=mask_seq_ps[:], func=ACT.Copy, accum_out=mask_and_sum[:, L:]
+        )
         logs = held.tile([B, L + 1], F32, name="logs")
         nc.scalar.activation(out=logs[:], in_=mask_and_sum[:], func=ACT.Ln)
         mean_weight = held.tile([B, 1], F32, name="mean_weight")
         nc.scalar.activation(out=mean_weight[:], in_=logs[:, L:], func=ACT.Exp, scale=-1.0)
         log_mask = held.tile([B, NC, L], F32, name="log_mask", tag="values_place0")
-        nc.vector.tensor_tensor(log_mask[:], foreign[:], logs[:, :L].unsqueeze(1).to_broadcast([B, NC, L]), ALU.add)
-        mean_wide = ring.tile([B, NC, L], F32, name="mean_wide", tag="e_k", bufs=NI + 1)
-        nc.vector.tensor_scalar_mul(mean_wide[:], slot_wide, mean_weight[:])
+        for c in range(NC):
+            nc.scalar.activation(
+                out=log_mask[:, c, :], in_=logs[:, :L], func=ACT.Identity, bias=foreign[:, c : c + 1]
+            )
+        mean_wide = held.tile([B, NC, L], F32, name="mean_wide")
+        nc.scalar.activation(
+            out=mean_wide[:], in_=slot[:].unsqueeze(2).to_broadcast([B, NC, L]), func=ACT.Copy, scale=mean_weight[:]
+        )
+
+        ksum_padded = held.tile([P, NI * DIAG], F32, name="ksum_padded", tag="ksum_place")
+        nc.gpsimd.memset(ksum_padded[:], 0.0)
 
         def look_up_into(e, name, first):
             end = first + e.shape[1]
@@ -112,7 +125,7 @@ def tile_scaleddpattention_kernel(tc, tab, mask, wdec, offs, out):
             return look_up_into(ring.tile([P, PIECE], F32, name=f"e_{name}", bufs=bufs), name, i * PIECE)
 
         for i in range(NI):
-            k = look_up("k", i, NI + 1)
+            k = look_up("k", i, NI)
             for jc in range(NJ * NC):
                 j, c = divmod(jc, NC)
                 at = i * DIAG + j * TILE + c

@@ -21,6 +21,7 @@ NC = BLOCK // L
 TILE = P // NJ
 DIAG = NJ * TILE + NC
 PART_BLOCKS = [3, 3, 4, 4, 4, 4, 4, 4, 2]
+FIRST = BLOCK
 PLACES = 3
 LN_EPS = 1e-5
 BIG = 1e30
@@ -49,9 +50,8 @@ def tile_scaleddpattention_kernel(tc, tab, mask, wdec, offs, out):
         for name in ("v", "k", "q"):
             table[name] = held.tile([P, S], F32, name=f"table_{name}")
 
-        def load_mask_piece(i):
-            piece = slice(i * PIECE, (i + 1) * PIECE)
-            nc.sync.dma_start(mask_bc[:, piece], mask_row[piece].partition_broadcast(P))
+        def load_mask(first, end):
+            nc.sync.dma_start(mask_bc[:, first:end], mask_row[first:end].partition_broadcast(P))
 
         def load_table(name, first_row):
             half = S // 2
@@ -60,10 +60,11 @@ def tile_scaleddpattention_kernel(tc, tab, mask, wdec, offs, out):
 
         mask_by_seq = held.tile([B, L], F32, name="mask_by_seq")
         nc.sync.dma_start(mask_by_seq[:], mask.rearrange("o (b t) -> (o b) t", t=L))
-        load_mask_piece(0)
+        load_mask(0, FIRST)
         load_table("k", P)
+        load_mask(FIRST, PIECE)
         for i in range(1, NI):
-            load_mask_piece(i)
+            load_mask(i * PIECE, (i + 1) * PIECE)
         load_table("q", 2 * P)
         load_table("v", 0)
         wdec_sb = held.tile([P, P], BF16, name="wdec_sb")
@@ -72,48 +73,43 @@ def tile_scaleddpattention_kernel(tc, tab, mask, wdec, offs, out):
         ident = held.tile([P, P], F32, name="ident")
         make_identity(nc, ident[:])
         ident_bf = held.tile([P, P], BF16, name="ident_bf")
-        nc.scalar.copy(ident_bf[:], ident[:])
+        nc.gpsimd.tensor_copy(ident_bf[:], ident[:])
         to_row = held.tile([B, B], F32, name="to_row")
-        nc.scalar.copy(
-            to_row[:].rearrange("b (j i c) -> b i j c", i=NI, c=NC),
-            ident[:].rearrange("b (i j c) -> b i j c", j=NJ, c=NC),
+        nc.gpsimd.tensor_copy(
+            to_row[:].rearrange("b (j i c) -> b j i c", j=NJ, c=NC),
+            ident[:].rearrange("b (i j c) -> b j i c", j=NJ, c=NC),
         )
-        slot = held.tile([B, NC], F32, name="slot", tag="ksum_place")
-        every_nc = held.tile([B, B // NC], F32, name="every_nc")
-        for c in range(NC):
-            nc.scalar.activation(
-                out=every_nc[:],
-                in_=ident[:].rearrange("p (k c) -> p c k", c=NC)[:, c, :],
-                func=ACT.Copy,
-                accum_out=slot[:, c : c + 1],
-            )
+        slot = ident
+        width = B // 2
+        while width >= NC:
+            folded = held.tile([B, width], F32, name=f"folded_{width}")
+            nc.gpsimd.tensor_tensor(folded[:], slot[:, :width], slot[:, width : 2 * width], ALU.add)
+            slot, width = folded, width // 2
         foreign = held.tile([B, NC], F32, name="foreign")
-        nc.scalar.activation(out=foreign[:], in_=slot[:], func=ACT.Copy, scale=BIG, bias=-BIG)
+        nc.gpsimd.tensor_scalar(foreign[:], slot[:], BIG, -BIG, op0=ALU.mult, op1=ALU.add)
+        ksum_padded = held.tile([P, NI * DIAG], F32, name="ksum_padded")
+        nc.vector.memset(ksum_padded[:], 0.0)
         pool_padded = held.tile([P, NI * DIAG], F32, name="pool_padded")
         nc.vector.memset(pool_padded[:], 0.0)
+        minus_one = held.tile([B, 1], F32, name="minus_one", tag="values_place0")
+        nc.vector.memset(minus_one[:], -1.0)
 
-        mask_seq_ps = psum_held.tile([B, L], F32, name="mask_seq_ps")
-        nc.tensor.matmul(mask_seq_ps[:], lhsT=to_row[:], rhs=mask_by_seq[:], start=True, stop=True)
-        mask_and_sum = held.tile([B, L + 1], F32, name="mask_and_sum")
-        nc.scalar.activation(
-            out=mask_and_sum[:, :L], in_=mask_seq_ps[:], func=ACT.Copy, accum_out=mask_and_sum[:, L:]
-        )
-        logs = held.tile([B, L + 1], F32, name="logs")
-        nc.scalar.activation(out=logs[:], in_=mask_and_sum[:], func=ACT.Ln)
+        mask_sum = held.tile([B, 1], F32, name="mask_sum")
+        nc.vector.reduce_sum(out=mask_sum[:], in_=mask_by_seq[:], axis=AX.X)
+        log_sum = held.tile([B, 1], F32, name="log_sum")
+        nc.scalar.activation(out=log_sum[:], in_=mask_sum[:], func=ACT.Ln)
+        log_mask = held.tile([B, L], F32, name="log_mask")
+        nc.scalar.activation(out=log_mask[:], in_=mask_by_seq[:], func=ACT.Ln)
         mean_weight = held.tile([B, 1], F32, name="mean_weight")
-        nc.scalar.activation(out=mean_weight[:], in_=logs[:, L:], func=ACT.Exp, scale=-1.0)
-        log_mask = held.tile([B, NC, L], F32, name="log_mask", tag="values_place0")
-        for c in range(NC):
-            nc.scalar.activation(
-                out=log_mask[:, c, :], in_=logs[:, :L], func=ACT.Identity, bias=foreign[:, c : c + 1]
-            )
-        mean_wide = held.tile([B, NC, L], F32, name="mean_wide")
-        nc.scalar.activation(
-            out=mean_wide[:], in_=slot[:].unsqueeze(2).to_broadcast([B, NC, L]), func=ACT.Copy, scale=mean_weight[:]
-        )
+        nc.scalar.activation(out=mean_weight[:], in_=log_sum[:], func=ACT.Exp, scale=-1.0)
+        mean_slot = held.tile([B, NC], F32, name="mean_slot")
+        nc.gpsimd.tensor_scalar_mul(mean_slot[:], slot[:], mean_weight[:])
 
-        ksum_padded = held.tile([P, NI * DIAG], F32, name="ksum_padded", tag="ksum_place")
-        nc.gpsimd.memset(ksum_padded[:], 0.0)
+        def over_tokens(per_slot):
+            return per_slot[:].unsqueeze(2).to_broadcast([B, NC, L])
+
+        mean_ps = psum_held.tile([B, NC, L], F32, name="mean_ps")
+        nc.tensor.matmul(mean_ps[:], lhsT=to_row[:], rhs=over_tokens(mean_slot), start=True, stop=True)
 
         def look_up_into(e, name, first):
             end = first + e.shape[1]
@@ -124,24 +120,38 @@ def tile_scaleddpattention_kernel(tc, tab, mask, wdec, offs, out):
         def look_up(name, i, bufs):
             return look_up_into(ring.tile([P, PIECE], F32, name=f"e_{name}", bufs=bufs), name, i * PIECE)
 
-        for i in range(NI):
-            k = look_up("k", i, NI)
-            for jc in range(NJ * NC):
-                j, c = divmod(jc, NC)
+        first_part = look_up_into(held.tile([P, FIRST], F32, name="e_k_first"), "k", 0)
+        second_part = look_up_into(held.tile([P, PIECE - FIRST], F32, name="e_k_second"), "k", FIRST)
+        for k, first in [(first_part, 0), (second_part, FIRST)] + [(None, i * PIECE) for i in range(1, NI)]:
+            if k is None:
+                k = look_up("k", first // PIECE, NI - 1)
+            for n in range(k.shape[1] // L):
+                i, j, c = (first // L + n) // (NJ * NC), (first // L + n) // NC % NJ, n % NC
                 at = i * DIAG + j * TILE + c
-                seq = k[:, jc * L : (jc + 1) * L]
-                nc.scalar.activation(out=seq, in_=seq, func=ACT.Copy, accum_out=ksum_padded[:, at : at + 1])
+                seq = k[:, n * L : (n + 1) * L]
+                nc.scalar.activation(
+                    out=seq,
+                    in_=seq,
+                    func=ACT.Copy,
+                    scale=1.0 / math.sqrt(P),
+                    accum_out=ksum_padded[:, at : at + 1],
+                )
 
-        cross_ps = psum_held.tile([B, BLOCK], F32, name="cross_ps", tag="bank0")
+        cross_ps = psum_held.tile([B, NC, L], F32, name="cross_ps", tag="bank0")
+        for j in range(NJ):
+            rows = slice(j * TILE, (j + 1) * TILE)
+            log_mask_wide = log_mask[:].unsqueeze(1).to_broadcast([B, NC, L])
+            nc.tensor.matmul(cross_ps[rows], lhsT=to_row[:, rows], rhs=log_mask_wide, start=True, stop=False)
+            nc.tensor.matmul(cross_ps[rows], lhsT=to_row[:, rows], rhs=over_tokens(foreign), start=False, stop=False)
         for i in range(NI):
-            q = look_up("q", i, 3)
+            q = look_up("q", i, NI)
             for j in range(NJ):
                 block = i * NJ + j
                 nc.tensor.matmul(
-                    cross_ps[j * TILE : (j + 1) * TILE, :],
+                    cross_ps[j * TILE : (j + 1) * TILE].rearrange("r c t -> r (c t)"),
                     lhsT=ksum_padded[:, block * TILE : (block + 1) * TILE],
                     rhs=q[:, j * BLOCK : (j + 1) * BLOCK],
-                    start=(i == 0),
+                    start=False,
                     stop=(i == NI - 1),
                 )
 
@@ -150,24 +160,26 @@ def tile_scaleddpattention_kernel(tc, tab, mask, wdec, offs, out):
         eps_row = held.tile([B, 1], F32, name="eps_row")
 
         def scores_to_exp():
-            score = held.tile([B, BLOCK], F32, name="score")
-            nc.vector.scalar_tensor_tensor(
-                out=score[:],
-                in0=cross_ps[:],
-                scalar=1.0 / math.sqrt(P),
-                in1=log_mask[:].rearrange("r c t -> r (c t)"),
-                op0=ALU.mult,
-                op1=ALU.add,
-            )
+            negated = held.tile([B, BLOCK], F32, name="negated")
             neg_max = held.tile([B, 1], F32, name="neg_max")
-            nc.vector.reduce_max(out=neg_max[:], in_=score[:], axis=AX.X, negate=True)
-            nc.scalar.activation(out=y[:], in_=score[:], func=ACT.Exp, bias=neg_max[:], scale=1.0, accum_out=y_sum[:])
+            nc.vector.tensor_scalar(
+                out=negated[:],
+                in0=cross_ps[:].rearrange("r c t -> r (c t)"),
+                scalar1=minus_one[:],
+                scalar2=None,
+                op0=ALU.mult,
+                op1=ALU.min,
+                accum_out=neg_max[:],
+            )
+            nc.scalar.activation(
+                out=y[:], in_=negated[:], func=ACT.Exp, bias=neg_max[:], scale=-1.0, accum_out=y_sum[:]
+            )
 
         def exp_to_weights():
             pool_wide = held.tile([B, P], F32, name="pool_wide", tag="values_place2")
             nc.vector.scalar_tensor_tensor(
                 out=pool_wide[:],
-                in0=mean_wide[:].rearrange("b c t -> b (c t)"),
+                in0=mean_ps[:].rearrange("b c t -> b (c t)"),
                 scalar=y_sum[:],
                 in1=y[:],
                 op0=ALU.mult,

@@ -20,7 +20,7 @@ NJ = PIECE // BLOCK
 NC = BLOCK // L
 TILE = P // NJ
 DIAG = NJ * TILE + NC
-PART_BLOCKS = [3, 3, 4, 4, 4, 4, 4, 4, 2]
+PART_BLOCKS = [4, 3, 4, 4, 4, 4, 4, 3, 2]
 FIRST = BLOCK
 PLACES = 3
 LN_EPS = 1e-5
@@ -45,13 +45,15 @@ def tile_scaleddpattention_kernel(tc, tab, mask, wdec, offs, out):
         nc.sync.dma_start(offsets[:], offs)
 
         mask_row = mask.rearrange("o n -> (o n)")
+        mask_first = held.tile([P, PIECE], F32, name="mask_first", tag="mask_first")
         mask_bc = held.tile([P, N], F32, name="mask_bc")
         table = {}
         for name in ("v", "k", "q"):
             table[name] = held.tile([P, S], F32, name=f"table_{name}")
 
         def load_mask(first, end):
-            nc.sync.dma_start(mask_bc[:, first:end], mask_row[first:end].partition_broadcast(P))
+            mask_tile = mask_first if first < PIECE else mask_bc
+            nc.sync.dma_start(mask_tile[:, first:end], mask_row[first:end].partition_broadcast(P))
 
         def load_table(name, first_row):
             half = S // 2
@@ -72,49 +74,47 @@ def tile_scaleddpattention_kernel(tc, tab, mask, wdec, offs, out):
 
         ident = held.tile([P, P], F32, name="ident")
         make_identity(nc, ident[:])
-        ident_bf = held.tile([P, P], BF16, name="ident_bf")
-        nc.gpsimd.tensor_copy(ident_bf[:], ident[:])
         to_row = held.tile([B, B], F32, name="to_row")
-        nc.gpsimd.tensor_copy(
+        nc.scalar.copy(
             to_row[:].rearrange("b (j i c) -> b j i c", j=NJ, c=NC),
             ident[:].rearrange("b (i j c) -> b j i c", j=NJ, c=NC),
         )
-        slot = ident
-        width = B // 2
-        while width >= NC:
-            folded = held.tile([B, width], F32, name=f"folded_{width}")
-            nc.gpsimd.tensor_tensor(folded[:], slot[:, :width], slot[:, width : 2 * width], ALU.add)
-            slot, width = folded, width // 2
-        foreign = held.tile([B, NC], F32, name="foreign")
-        nc.gpsimd.tensor_scalar(foreign[:], slot[:], BIG, -BIG, op0=ALU.mult, op1=ALU.add)
+        pool_padded = held.tile([P, NI * DIAG], F32, name="pool_padded")
+        nc.gpsimd.memset(pool_padded[:], 0.0)
         ksum_padded = held.tile([P, NI * DIAG], F32, name="ksum_padded")
         nc.vector.memset(ksum_padded[:], 0.0)
-        pool_padded = held.tile([P, NI * DIAG], F32, name="pool_padded")
-        nc.vector.memset(pool_padded[:], 0.0)
         minus_one = held.tile([B, 1], F32, name="minus_one", tag="values_place0")
         nc.vector.memset(minus_one[:], -1.0)
+        stripes = held.tile([B, NC, L], F32, name="stripes", align_bytes=64)
+        nc.vector.memset(stripes[:], 0.0)
+        for c in range(NC):
+            nc.vector.memset(stripes[:, c, c:L:NC], 1.0)
+        slot = held.tile([B, NC, L], F32, name="slot", align_bytes=64)
+        nc.vector.transpose(slot[:].rearrange("b c t -> b (c t)"), stripes[:].rearrange("b c t -> b (c t)"))
+        foreign = held.tile([B, NC, L], F32, name="foreign")
+        nc.vector.tensor_scalar(foreign[:], slot[:], 1.0, BIG, op0=ALU.subtract, op1=ALU.mult)
 
         mask_sum = held.tile([B, 1], F32, name="mask_sum")
         nc.vector.reduce_sum(out=mask_sum[:], in_=mask_by_seq[:], axis=AX.X)
-        log_sum = held.tile([B, 1], F32, name="log_sum")
-        nc.scalar.activation(out=log_sum[:], in_=mask_sum[:], func=ACT.Ln)
         log_mask = held.tile([B, L], F32, name="log_mask")
         nc.scalar.activation(out=log_mask[:], in_=mask_by_seq[:], func=ACT.Ln)
+        log_sum = held.tile([B, 1], F32, name="log_sum")
+        nc.scalar.activation(out=log_sum[:], in_=mask_sum[:], func=ACT.Ln)
         mean_weight = held.tile([B, 1], F32, name="mean_weight")
         nc.scalar.activation(out=mean_weight[:], in_=log_sum[:], func=ACT.Exp, scale=-1.0)
-        mean_slot = held.tile([B, NC], F32, name="mean_slot")
-        nc.gpsimd.tensor_scalar_mul(mean_slot[:], slot[:], mean_weight[:])
-
-        def over_tokens(per_slot):
-            return per_slot[:].unsqueeze(2).to_broadcast([B, NC, L])
+        mean_wide = held.tile([B, NC, L], F32, name="mean_wide")
+        nc.scalar.activation(out=mean_wide[:], in_=slot[:], func=ACT.Copy, scale=mean_weight[:])
+        log_wide = held.tile([B, NC, L], F32, name="log_wide")
+        nc.vector.tensor_tensor(log_wide[:], foreign[:], log_mask[:].unsqueeze(1).to_broadcast([B, NC, L]), ALU.add)
 
         mean_ps = psum_held.tile([B, NC, L], F32, name="mean_ps")
-        nc.tensor.matmul(mean_ps[:], lhsT=to_row[:], rhs=over_tokens(mean_slot), start=True, stop=True)
+        nc.tensor.matmul(mean_ps[:], lhsT=to_row[:], rhs=mean_wide[:], start=True, stop=True)
 
         def look_up_into(e, name, first):
             end = first + e.shape[1]
             picked = table[name][:].indirect(offsets[:, first // 16 : end // 16])
-            nc.vector.tensor_tensor(e[:], picked, mask_bc[:, first:end], ALU.mult)
+            mask_tile = mask_first if first < PIECE else mask_bc
+            nc.vector.tensor_tensor(e[:], picked, mask_tile[:, first:end], ALU.mult)
             return e
 
         def look_up(name, i, bufs):
@@ -140,9 +140,7 @@ def tile_scaleddpattention_kernel(tc, tab, mask, wdec, offs, out):
         cross_ps = psum_held.tile([B, NC, L], F32, name="cross_ps", tag="bank0")
         for j in range(NJ):
             rows = slice(j * TILE, (j + 1) * TILE)
-            log_mask_wide = log_mask[:].unsqueeze(1).to_broadcast([B, NC, L])
-            nc.tensor.matmul(cross_ps[rows], lhsT=to_row[:, rows], rhs=log_mask_wide, start=True, stop=False)
-            nc.tensor.matmul(cross_ps[rows], lhsT=to_row[:, rows], rhs=over_tokens(foreign), start=False, stop=False)
+            nc.tensor.matmul(cross_ps[rows], lhsT=to_row[:, rows], rhs=log_wide[:], start=True, stop=False)
         for i in range(NI):
             q = look_up("q", i, NI)
             for j in range(NJ):
@@ -160,7 +158,7 @@ def tile_scaleddpattention_kernel(tc, tab, mask, wdec, offs, out):
         eps_row = held.tile([B, 1], F32, name="eps_row")
 
         def scores_to_exp():
-            negated = held.tile([B, BLOCK], F32, name="negated")
+            negated = held.tile([B, BLOCK], F32, name="negated", tag="mask_first")
             neg_max = held.tile([B, 1], F32, name="neg_max")
             nc.vector.tensor_scalar(
                 out=negated[:],
@@ -241,10 +239,10 @@ def tile_scaleddpattention_kernel(tc, tab, mask, wdec, offs, out):
         nc.vector.bn_aggr(mean_var[:], stats[:])
         rstd = held.tile([B, 1], F32, name="rstd")
         nc.scalar.activation(out=rstd[:], in_=mean_var[:, 1:2], func=ACT.Abs_reciprocal_sqrt, bias=eps_row[:], scale=1.0)
-        zT = held.tile([B, P], BF16, name="zT")
+        zT = held.tile([B, P], F32, name="zT")
         nc.vector.tensor_scalar(zT[:], h_ps[:], mean_var[:, 0:1], rstd[:], op0=ALU.subtract, op1=ALU.mult)
-        z_ps = psum_held.tile([P, B], BF16, name="z_ps")
-        nc.tensor.transpose(z_ps[:], zT[:], ident_bf[:])
+        z_ps = psum_held.tile([P, B], F32, name="z_ps")
+        nc.tensor.transpose(z_ps[:], zT[:], ident[:])
         z = held.tile([P, B], BF16, name="z")
         nc.vector.tensor_copy(z[:], z_ps[:])
         out_ps = psum_held.tile([P, B], F32, name="out_ps")

@@ -22,6 +22,7 @@ TILE = P // NJ
 DIAG = NJ * TILE + NC
 PART_BLOCKS = [4, 3, 4, 4, 4, 4, 4, 3, 2]
 FIRST = BLOCK
+SPREAD = 5
 PLACES = 3
 LN_EPS = 1e-5
 BIG = 1e30
@@ -62,11 +63,15 @@ def tile_scaleddpattention_kernel(tc, tab, mask, wdec, offs, out):
 
         mask_by_seq = held.tile([B, L], F32, name="mask_by_seq")
         nc.sync.dma_start(mask_by_seq[:], mask.rearrange("o (b t) -> (o b) t", t=L))
+        mask_rows = held.tile([P, PIECE], F32, name="mask_rows")
+        nc.gpsimd.memset(mask_rows[:], 0.0)
         load_mask(0, FIRST)
         load_table("k", P)
         load_mask(FIRST, PIECE)
-        for i in range(1, NI):
-            load_mask(i * PIECE, (i + 1) * PIECE)
+        nc.sync.dma_start(mask_rows[: NI - SPREAD, :], mask.rearrange("o (i n) -> (o i) n", n=PIECE)[SPREAD:, :])
+        load_mask(PIECE, 2 * PIECE)
+        load_mask(2 * PIECE, 3 * PIECE)
+        load_mask(3 * PIECE, SPREAD * PIECE)
         load_table("q", 2 * P)
         load_table("v", 0)
         wdec_sb = held.tile([P, P], BF16, name="wdec_sb")
@@ -74,6 +79,13 @@ def tile_scaleddpattention_kernel(tc, tab, mask, wdec, offs, out):
 
         ident = held.tile([P, P], F32, name="ident")
         make_identity(nc, ident[:])
+        for i in range(SPREAD, NI):
+            row = i - SPREAD
+            spread_ps = psum_held.tile([P, PIECE], F32, name="spread_ps")
+            nc.tensor.matmul(
+                spread_ps[:], lhsT=ident[:, row : row + 1].to_broadcast([P, P]), rhs=mask_rows[:], start=True, stop=True
+            )
+            nc.scalar.copy(mask_bc[:, i * PIECE : (i + 1) * PIECE], spread_ps[:])
         to_row = held.tile([B, B], F32, name="to_row")
         nc.scalar.copy(
             to_row[:].rearrange("b (j i c) -> b j i c", j=NJ, c=NC),

@@ -23,6 +23,7 @@ DIAG = NJ * TILE + NC
 PART_BLOCKS = [4, 3, 4, 4, 4, 4, 4, 3, 2]
 FIRST = BLOCK
 SPREAD = 5
+STEP = 32
 PLACES = 3
 LN_EPS = 1e-5
 BIG = 1e30
@@ -65,10 +66,14 @@ def tile_scaleddpattention_kernel(tc, tab, mask, wdec, offs, out):
         nc.sync.dma_start(mask_by_seq[:], mask.rearrange("o (b t) -> (o b) t", t=L))
         mask_rows = held.tile([P, PIECE], F32, name="mask_rows")
         nc.gpsimd.memset(mask_rows[:], 0.0)
+        select = held.tile([P, NI - SPREAD], F32, name="select")
+        nc.vector.memset(select[:], 0.0)
+        for n in range(NI - SPREAD):
+            nc.vector.memset(select[n * STEP : n * STEP + 1, n : n + 1], 1.0)
         load_mask(0, FIRST)
         load_table("k", P)
         load_mask(FIRST, PIECE)
-        nc.sync.dma_start(mask_rows[: NI - SPREAD, :], mask.rearrange("o (i n) -> (o i) n", n=PIECE)[SPREAD:, :])
+        nc.sync.dma_start(mask_rows[: (NI - SPREAD) * STEP : STEP, :], mask.rearrange("o (i n) -> (o i) n", n=PIECE)[SPREAD:, :])
         load_mask(PIECE, 2 * PIECE)
         load_mask(2 * PIECE, 3 * PIECE)
         load_mask(3 * PIECE, SPREAD * PIECE)
@@ -79,15 +84,15 @@ def tile_scaleddpattention_kernel(tc, tab, mask, wdec, offs, out):
 
         ident = held.tile([P, P], F32, name="ident")
         make_identity(nc, ident[:])
-        for i in range(SPREAD, NI):
-            row = i - SPREAD
-            spread_ps = psum_held.tile([P, PIECE], F32, name="spread_ps")
+        for n in range(NI - SPREAD):
+            piece = slice((SPREAD + n) * PIECE, (SPREAD + n + 1) * PIECE)
+            spread_ps = psum_held.tile([P, PIECE], F32, name="spread_ps", bufs=2)
             nc.tensor.matmul(
-                spread_ps[:], lhsT=ident[:, row : row + 1].to_broadcast([P, P]), rhs=mask_rows[:], start=True, stop=True
+                spread_ps[:], lhsT=select[:, n : n + 1].to_broadcast([P, P]), rhs=mask_rows[:], start=True, stop=True
             )
-            nc.scalar.copy(mask_bc[:, i * PIECE : (i + 1) * PIECE], spread_ps[:])
+            nc.scalar.copy(mask_bc[:, piece], spread_ps[:])
         to_row = held.tile([B, B], F32, name="to_row")
-        nc.scalar.copy(
+        nc.gpsimd.tensor_copy(
             to_row[:].rearrange("b (j i c) -> b j i c", j=NJ, c=NC),
             ident[:].rearrange("b (i j c) -> b j i c", j=NJ, c=NC),
         )

@@ -53,9 +53,9 @@ def tile_scaleddpattention_kernel(tc, tab, mask, wdec, offs, out):
         for name in ("v", "k", "q"):
             table[name] = held.tile([P, S], F32, name=f"table_{name}")
 
-        def load_mask(first, end):
+        def load_mask(first, end, queue=nc.sync):
             mask_tile = mask_first if first < PIECE else mask_bc
-            nc.sync.dma_start(mask_tile[:, first:end], mask_row[first:end].partition_broadcast(P))
+            queue.dma_start(mask_tile[:, first:end], mask_row[first:end].partition_broadcast(P))
 
         def load_table(name, first_row):
             half = S // 2
@@ -63,14 +63,14 @@ def tile_scaleddpattention_kernel(tc, tab, mask, wdec, offs, out):
             nc.sync.dma_start(table[name][:, half:], tab[first_row : first_row + P, half:])
 
         mask_by_seq = held.tile([B, L], F32, name="mask_by_seq")
-        nc.sync.dma_start(mask_by_seq[:], mask.rearrange("o (b t) -> (o b) t", t=L))
+        nc.scalar.dma_start(mask_by_seq[:], mask.rearrange("o (b t) -> (o b) t", t=L))
         mask_rows = held.tile([P, PIECE], F32, name="mask_rows")
         nc.gpsimd.memset(mask_rows[:], 0.0)
         select = held.tile([P, NI - SPREAD], F32, name="select")
         nc.vector.memset(select[:], 0.0)
         for n in range(NI - SPREAD):
             nc.vector.memset(select[n * STEP : n * STEP + 1, n : n + 1], 1.0)
-        load_mask(0, FIRST)
+        load_mask(0, FIRST, nc.scalar)
         load_table("k", P)
         load_mask(FIRST, PIECE)
         nc.sync.dma_start(mask_rows[: (NI - SPREAD) * STEP : STEP, :], mask.rearrange("o (i n) -> (o i) n", n=PIECE)[SPREAD:, :])
@@ -121,9 +121,6 @@ def tile_scaleddpattention_kernel(tc, tab, mask, wdec, offs, out):
         nc.scalar.activation(out=mean_weight[:], in_=log_sum[:], func=ACT.Exp, scale=-1.0)
         mean_wide = held.tile([B, NC, L], F32, name="mean_wide")
         nc.scalar.activation(out=mean_wide[:], in_=slot[:], func=ACT.Copy, scale=mean_weight[:])
-        log_wide = held.tile([B, NC, L], F32, name="log_wide")
-        nc.vector.tensor_tensor(log_wide[:], foreign[:], log_mask[:].unsqueeze(1).to_broadcast([B, NC, L]), ALU.add)
-
         mean_ps = psum_held.tile([B, NC, L], F32, name="mean_ps")
         nc.tensor.matmul(mean_ps[:], lhsT=to_row[:], rhs=mean_wide[:], start=True, stop=True)
 
@@ -157,7 +154,9 @@ def tile_scaleddpattention_kernel(tc, tab, mask, wdec, offs, out):
         cross_ps = psum_held.tile([B, NC, L], F32, name="cross_ps", tag="bank0")
         for j in range(NJ):
             rows = slice(j * TILE, (j + 1) * TILE)
-            nc.tensor.matmul(cross_ps[rows], lhsT=to_row[:, rows], rhs=log_wide[:], start=True, stop=False)
+            log_mask_wide = log_mask[:].unsqueeze(1).to_broadcast([B, NC, L])
+            nc.tensor.matmul(cross_ps[rows], lhsT=to_row[:, rows], rhs=foreign[:], start=True, stop=False)
+            nc.tensor.matmul(cross_ps[rows], lhsT=to_row[:, rows], rhs=log_mask_wide, start=False, stop=False)
         for i in range(NI):
             q = look_up("q", i, NI)
             for j in range(NJ):

@@ -22,6 +22,8 @@ TILE = P // NJ
 DIAG = NJ * TILE + NC
 PART_BLOCKS = [4, 3, 4, 4, 4, 4, 4, 3, 2]
 FIRST = BLOCK
+KEY_PARTS = [FIRST, PIECE - FIRST, PIECE] + 3 * [2 * PIECE]
+QUERY_PARTS = [PIECE] + 3 * [2 * PIECE] + [PIECE]
 SPREAD = 5
 STEP = 32
 PLACES = 3
@@ -74,9 +76,8 @@ def tile_scaleddpattention_kernel(tc, tab, mask, wdec, offs, out):
         load_table("k", P)
         load_mask(FIRST, PIECE)
         nc.sync.dma_start(mask_rows[: (NI - SPREAD) * STEP : STEP, :], mask.rearrange("o (i n) -> (o i) n", n=PIECE)[SPREAD:, :])
-        load_mask(PIECE, 2 * PIECE)
-        load_mask(2 * PIECE, 3 * PIECE)
-        load_mask(3 * PIECE, SPREAD * PIECE)
+        for i in range(1, SPREAD):
+            load_mask(i * PIECE, (i + 1) * PIECE)
         load_table("q", 2 * P)
         load_table("v", 0)
         wdec_sb = held.tile([P, P], BF16, name="wdec_sb")
@@ -131,16 +132,15 @@ def tile_scaleddpattention_kernel(tc, tab, mask, wdec, offs, out):
             nc.vector.tensor_tensor(e[:], picked, mask_tile[:, first:end], ALU.mult)
             return e
 
-        def look_up(name, i, bufs):
-            return look_up_into(ring.tile([P, PIECE], F32, name=f"e_{name}", bufs=bufs), name, i * PIECE)
+        def look_up(name, first, tokens):
+            return look_up_into(held.tile([P, tokens], F32, name=f"e_{name}_{first}"), name, first)
 
-        first_part = look_up_into(held.tile([P, FIRST], F32, name="e_k_first"), "k", 0)
-        second_part = look_up_into(held.tile([P, PIECE - FIRST], F32, name="e_k_second"), "k", FIRST)
-        for k, first in [(first_part, 0), (second_part, FIRST)] + [(None, i * PIECE) for i in range(1, NI)]:
-            if k is None:
-                k = look_up("k", first // PIECE, NI - 1)
-            for n in range(k.shape[1] // L):
-                i, j, c = (first // L + n) // (NJ * NC), (first // L + n) // NC % NJ, n % NC
+        first = 0
+        for tokens in KEY_PARTS:
+            k = look_up("k", first, tokens)
+            for n in range(tokens // L):
+                block, c = divmod(first // L + n, NC)
+                i, j = divmod(block, NJ)
                 at = i * DIAG + j * TILE + c
                 seq = k[:, n * L : (n + 1) * L]
                 nc.scalar.activation(
@@ -150,6 +150,7 @@ def tile_scaleddpattention_kernel(tc, tab, mask, wdec, offs, out):
                     scale=1.0 / math.sqrt(P),
                     accum_out=ksum_padded[:, at : at + 1],
                 )
+            first += tokens
 
         cross_ps = psum_held.tile([B, NC, L], F32, name="cross_ps", tag="bank0")
         for j in range(NJ):
@@ -157,17 +158,20 @@ def tile_scaleddpattention_kernel(tc, tab, mask, wdec, offs, out):
             log_mask_wide = log_mask[:].unsqueeze(1).to_broadcast([B, NC, L])
             nc.tensor.matmul(cross_ps[rows], lhsT=to_row[:, rows], rhs=foreign[:], start=True, stop=False)
             nc.tensor.matmul(cross_ps[rows], lhsT=to_row[:, rows], rhs=log_mask_wide, start=False, stop=False)
-        for i in range(NI):
-            q = look_up("q", i, NI)
-            for j in range(NJ):
-                block = i * NJ + j
+        first = 0
+        for tokens in QUERY_PARTS:
+            q = look_up("q", first, tokens)
+            for at in range(0, tokens, BLOCK):
+                block = (first + at) // BLOCK
+                i, j = divmod(block, NJ)
                 nc.tensor.matmul(
                     cross_ps[j * TILE : (j + 1) * TILE].rearrange("r c t -> r (c t)"),
                     lhsT=ksum_padded[:, block * TILE : (block + 1) * TILE],
-                    rhs=q[:, j * BLOCK : (j + 1) * BLOCK],
+                    rhs=q[:, at : at + BLOCK],
                     start=False,
                     stop=(i == NI - 1),
                 )
+            first += tokens
 
         y = held.tile([B, BLOCK], F32, name="y", tag="values_place1")
         y_sum = held.tile([B, 1], F32, name="y_sum")

import math

import concourse.mybir as mybir
from concourse.masks import make_identity

F32, BF16, U16 = mybir.dt.float32, mybir.dt.bfloat16, mybir.dt.uint16
ALU = mybir.AluOpType
ACT = mybir.ActivationFunctionType
AX = mybir.AxisListType

P = 128
S = 4096
N = 4096
L = 32
B = N // L
PIECE = 512
NI = N // PIECE
BLOCK = P
NJ = PIECE // BLOCK
NC = BLOCK // L
TILE = P // NJ
DIAG = NJ * TILE + NC
PART_BLOCKS = [4, 3, 4, 4, 4, 4, 4, 3, 2]
FIRST = BLOCK
KEY_PARTS = [FIRST, PIECE - FIRST, PIECE] + 3 * [2 * PIECE]
QUERY_PARTS = [PIECE] + 3 * [2 * PIECE] + [PIECE]
SPREAD = 5
STEP = 32
PLACES = 3
LN_EPS = 1e-5
BIG = 1e30

FLOPS = 2 * P * P * B + 2 * P * N + 2 * P * N


def own_columns(padded):
    by_piece = padded.rearrange("p (i s) -> p i s", s=DIAG)[:, :, : NJ * TILE]
    return by_piece.rearrange("p i (j r) -> p i j r", r=TILE)[:, :, :, :NC]


def tile_scaleddpattention_kernel(tc, tab, mask, wdec, offs, out):
    nc = tc.nc
    with (
        tc.tile_pool(name="held", bufs=1) as held,
        tc.tile_pool(name="ring", bufs=3) as ring,
        tc.psum_pool(name="psum_held", bufs=1) as psum_held,
    ):
        offsets = held.tile([P, N // 16], U16, name="offsets")
        nc.sync.dma_start(offsets[:], offs)

        mask_row = mask.rearrange("o n -> (o n)")
        mask_first = held.tile([P, PIECE], F32, name="mask_first", tag="mask_first")
        mask_bc = held.tile([P, N], F32, name="mask_bc")
        table = {}
        for name in ("v", "k", "q"):
            table[name] = held.tile([P, S], F32, name=f"table_{name}")

        def load_mask(first, end, queue=nc.sync):
            mask_tile = mask_first if first < PIECE else mask_bc
            queue.dma_start(mask_tile[:, first:end], mask_row[first:end].partition_broadcast(P))

        def load_table(name, first_row):
            half = S // 2
            nc.sync.dma_start(table[name][:, :half], tab[first_row : first_row + P, :half])
            nc.sync.dma_start(table[name][:, half:], tab[first_row : first_row + P, half:])

        mask_by_seq = held.tile([B, L], F32, name="mask_by_seq")
        nc.scalar.dma_start(mask_by_seq[:], mask.rearrange("o (b t) -> (o b) t", t=L))
        mask_rows = held.tile([P, PIECE], F32, name="mask_rows")
        nc.gpsimd.memset(mask_rows[:], 0.0)
        select = held.tile([P, NI - SPREAD], F32, name="select")
        nc.vector.memset(select[:], 0.0)
        for n in range(NI - SPREAD):
            nc.vector.memset(select[n * STEP : n * STEP + 1, n : n + 1], 1.0)
        load_mask(0, FIRST, nc.scalar)
        load_table("k", P)
        load_mask(FIRST, PIECE)
        nc.sync.dma_start(mask_rows[: (NI - SPREAD) * STEP : STEP, :], mask.rearrange("o (i n) -> (o i) n", n=PIECE)[SPREAD:, :])
        for i in range(1, SPREAD):
            load_mask(i * PIECE, (i + 1) * PIECE)
        load_table("q", 2 * P)
        load_table("v", 0)
        wdec_sb = held.tile([P, P], BF16, name="wdec_sb")
        nc.sync.dma_start(wdec_sb[:], wdec)

        ident = held.tile([P, P], F32, name="ident")
        make_identity(nc, ident[:])
        for n in range(NI - SPREAD):
            piece = slice((SPREAD + n) * PIECE, (SPREAD + n + 1) * PIECE)
            spread_ps = psum_held.tile([P, PIECE], F32, name="spread_ps", bufs=2)
            nc.tensor.matmul(
                spread_ps[:], lhsT=select[:, n : n + 1].to_broadcast([P, P]), rhs=mask_rows[:], start=True, stop=True
            )
            nc.scalar.copy(mask_bc[:, piece], spread_ps[:])
        to_row = held.tile([B, B], F32, name="to_row")
        nc.gpsimd.tensor_copy(
            to_row[:].rearrange("b (j i c) -> b j i c", j=NJ, c=NC),
            ident[:].rearrange("b (i j c) -> b j i c", j=NJ, c=NC),
        )
        pool_padded = held.tile([P, NI * DIAG], F32, name="pool_padded")
        nc.gpsimd.memset(pool_padded[:], 0.0)
        ksum_padded = held.tile([P, NI * DIAG], F32, name="ksum_padded")
        nc.vector.memset(ksum_padded[:], 0.0)
        minus_one = held.tile([B, 1], F32, name="minus_one", tag="values_place0")
        nc.vector.memset(minus_one[:], -1.0)
        stripes = held.tile([B, NC, L], F32, name="stripes", align_bytes=64)
        nc.vector.memset(stripes[:], 0.0)
        for c in range(NC):
            nc.vector.memset(stripes[:, c, c:L:NC], 1.0)
        slot = held.tile([B, NC, L], F32, name="slot", align_bytes=64)
        nc.vector.transpose(slot[:].rearrange("b c t -> b (c t)"), stripes[:].rearrange("b c t -> b (c t)"))
        foreign = held.tile([B, NC, L], F32, name="foreign")
        nc.vector.tensor_scalar(foreign[:], slot[:], 1.0, BIG, op0=ALU.subtract, op1=ALU.mult)

        mask_sum = held.tile([B, 1], F32, name="mask_sum")
        nc.vector.reduce_sum(out=mask_sum[:], in_=mask_by_seq[:], axis=AX.X)
        log_mask = held.tile([B, L], F32, name="log_mask")
        nc.scalar.activation(out=log_mask[:], in_=mask_by_seq[:], func=ACT.Ln)
        log_sum = held.tile([B, 1], F32, name="log_sum")
        nc.scalar.activation(out=log_sum[:], in_=mask_sum[:], func=ACT.Ln)
        mean_weight = held.tile([B, 1], F32, name="mean_weight")
        nc.scalar.activation(out=mean_weight[:], in_=log_sum[:], func=ACT.Exp, scale=-1.0)
        mean_wide = held.tile([B, NC, L], F32, name="mean_wide")
        nc.scalar.activation(out=mean_wide[:], in_=slot[:], func=ACT.Copy, scale=mean_weight[:])
        mean_ps = psum_held.tile([B, NC, L], F32, name="mean_ps")
        nc.tensor.matmul(mean_ps[:], lhsT=to_row[:], rhs=mean_wide[:], start=True, stop=True)

        def look_up_into(e, name, first):
            end = first + e.shape[1]
            picked = table[name][:].indirect(offsets[:, first // 16 : end // 16])
            mask_tile = mask_first if first < PIECE else mask_bc
            nc.vector.tensor_tensor(e[:], picked, mask_tile[:, first:end], ALU.mult)
            return e

        def look_up(name, first, tokens):
            return look_up_into(held.tile([P, tokens], F32, name=f"e_{name}_{first}"), name, first)

        first = 0
        for tokens in KEY_PARTS:
            k = look_up("k", first, tokens)
            for n in range(tokens // L):
                block, c = divmod(first // L + n, NC)
                i, j = divmod(block, NJ)
                at = i * DIAG + j * TILE + c
                seq = k[:, n * L : (n + 1) * L]
                nc.scalar.activation(
                    out=seq,
                    in_=seq,
                    func=ACT.Copy,
                    scale=1.0 / math.sqrt(P),
                    accum_out=ksum_padded[:, at : at + 1],
                )
            first += tokens

        cross_ps = psum_held.tile([B, NC, L], F32, name="cross_ps", tag="bank0")
        for j in range(NJ):
            rows = slice(j * TILE, (j + 1) * TILE)
            log_mask_wide = log_mask[:].unsqueeze(1).to_broadcast([B, NC, L])
            nc.tensor.matmul(cross_ps[rows], lhsT=to_row[:, rows], rhs=foreign[:], start=True, stop=False)
            nc.tensor.matmul(cross_ps[rows], lhsT=to_row[:, rows], rhs=log_mask_wide, start=False, stop=False)
        first = 0
        for tokens in QUERY_PARTS:
            q = look_up("q", first, tokens)
            for at in range(0, tokens, BLOCK):
                block = (first + at) // BLOCK
                i, j = divmod(block, NJ)
                nc.tensor.matmul(
                    cross_ps[j * TILE : (j + 1) * TILE].rearrange("r c t -> r (c t)"),
                    lhsT=ksum_padded[:, block * TILE : (block + 1) * TILE],
                    rhs=q[:, at : at + BLOCK],
                    start=False,
                    stop=(i == NI - 1),
                )
            first += tokens

        y = held.tile([B, BLOCK], F32, name="y", tag="values_place1")
        y_sum = held.tile([B, 1], F32, name="y_sum")
        eps_row = held.tile([B, 1], F32, name="eps_row")

        def scores_to_exp():
            negated = held.tile([B, BLOCK], F32, name="negated", tag="mask_first")
            neg_max = held.tile([B, 1], F32, name="neg_max")
            nc.vector.tensor_scalar(
                out=negated[:],
                in0=cross_ps[:].rearrange("r c t -> r (c t)"),
                scalar1=minus_one[:],
                scalar2=None,
                op0=ALU.mult,
                op1=ALU.min,
                accum_out=neg_max[:],
            )
            nc.scalar.activation(
                out=y[:], in_=negated[:], func=ACT.Exp, bias=neg_max[:], scale=-1.0, accum_out=y_sum[:]
            )

        def exp_to_weights():
            pool_wide = held.tile([B, P], F32, name="pool_wide", tag="values_place2")
            nc.vector.scalar_tensor_tensor(
                out=pool_wide[:],
                in0=mean_ps[:].rearrange("b c t -> b (c t)"),
                scalar=y_sum[:],
                in1=y[:],
                op0=ALU.mult,
                op1=ALU.add,
            )
            pool_ps = psum_held.tile([P, B], F32, name="pool_ps", tag="bank1")
            nc.tensor.transpose(pool_ps[:], pool_wide[:], ident[:])
            nc.scalar.copy(own_columns(pool_padded[:]), pool_ps[:].rearrange("p (j i c) -> p i j c", i=NI, c=NC))
            nc.scalar.activation(out=eps_row[:], in_=y_sum[:], func=ACT.Square, scale=math.sqrt(LN_EPS))

        h_ps = psum_held.tile([B, P], F32, name="h_ps")

        def look_up_values(part):
            place = "values_first" if part == 0 else f"values_place{(part - 1) % PLACES}"
            v = held.tile([P, PART_BLOCKS[part] * BLOCK], F32, name="e_v", tag=place)
            return look_up_into(v, "v", sum(PART_BLOCKS[:part]) * BLOCK)

        def flip(part, v):
            vT_ps = psum_held.tile([P, PIECE], F32, name="vT_ps", tag=f"bank{part % 2}")
            columns = PART_BLOCKS[part] * P
            for at in range(0, columns, P):
                nc.tensor.transpose(vT_ps[:, at : at + P], v[:, at : at + BLOCK], ident[:])
            vT = ring.tile([P, PIECE], F32, name="vT", bufs=len(PART_BLOCKS))
            copy = nc.vector.tensor_copy if part == len(PART_BLOCKS) - 1 else nc.scalar.copy
            copy(vT[:, :columns], vT_ps[:, :columns])
            return vT

        def pool_values(part, vT):
            for n in range(PART_BLOCKS[part]):
                block = sum(PART_BLOCKS[:part]) + n
                i, j = divmod(block, NJ)
                nc.tensor.matmul(
                    h_ps[j * TILE : (j + 1) * TILE, :],
                    lhsT=pool_padded[:, block * TILE : (block + 1) * TILE],
                    rhs=vT[:, n * P : (n + 1) * P],
                    start=(i == 0),
                    stop=(i == NI - 1),
                )

        v0 = look_up_values(0)
        scores_to_exp()
        vT = [flip(0, v0)]
        v1 = look_up_values(1)
        exp_to_weights()
        vT.append(flip(1, v1))
        pool_values(0, vT[0])
        vT.append(flip(2, look_up_values(2)))
        pool_values(1, vT[1])
        for part in range(3, len(PART_BLOCKS), 2):
            vT.append(flip(part, look_up_values(part)))
            vT.append(flip(part + 1, look_up_values(part + 1)))
            pool_values(part - 1, vT[part - 1])
            pool_values(part, vT[part])
        pool_values(part + 1, vT[part + 1])

        stats = held.tile([B, 6], F32, name="stats")
        nc.vector.bn_stats(stats[:], h_ps[:])
        mean_var = held.tile([B, 2], F32, name="mean_var")
        nc.vector.bn_aggr(mean_var[:], stats[:])
        rstd = held.tile([B, 1], F32, name="rstd")
        nc.scalar.activation(out=rstd[:], in_=mean_var[:, 1:2], func=ACT.Abs_reciprocal_sqrt, bias=eps_row[:], scale=1.0)
        zT = held.tile([B, P], F32, name="zT")
        nc.vector.tensor_scalar(zT[:], h_ps[:], mean_var[:, 0:1], rstd[:], op0=ALU.subtract, op1=ALU.mult)
        z_ps = psum_held.tile([P, B], F32, name="z_ps")
        nc.tensor.transpose(z_ps[:], zT[:], ident[:])
        z = held.tile([P, B], BF16, name="z")
        nc.vector.tensor_copy(z[:], z_ps[:])
        out_ps = psum_held.tile([P, B], F32, name="out_ps")
        nc.tensor.matmul(out_ps[:], lhsT=wdec_sb[:], rhs=z[:], start=True, stop=True)
        out_sb = held.tile([P, B], F32, name="out_sb")
        nc.vector.tensor_copy(
            out_sb[:].rearrange("m (i j c) -> m i j c", j=NJ, c=NC),
            out_ps[:].rearrange("m (j i c) -> m i j c", i=NI, c=NC),
        )
        nc.sync.dma_start(out, out_sb[:])
